import numpy as np
import ml_dtypes


def mxq(x, axis, fmt="e4m3"):
    dtype, down = {"e4m3": (ml_dtypes.float8_e4m3fn, 7), "e5m2": (ml_dtypes.float8_e5m2, 14)}[fmt]
    v = np.moveaxis(np.asarray(x, np.float32).astype(ml_dtypes.bfloat16).astype(np.float64), axis, -1)
    blocks = v.reshape(v.shape[:-1] + (-1, 32))
    amax = np.abs(blocks).max(-1, keepdims=True)
    byte = np.maximum(np.where(amax > 0, np.frexp(amax)[1] - 1 + 127, 0) - down, 1)
    scale = np.exp2(byte - 127.0)
    codes = (blocks / scale).astype(np.float32).astype(dtype).astype(np.float64)
    return np.moveaxis((codes * scale).reshape(v.shape), -1, axis)


WIDE = False


def mx_kscale(k):
    if not WIDE:
        return np.ones(k)
    levels = np.array([10, -10, 5, -5, 0])
    if k % 512:
        return np.exp2(np.random.permutation(np.resize(levels, k // 32))).repeat(32)
    a = np.empty((k // 512, 16))
    for p in range(k // 512):
        a[p, :8] = np.random.permutation(np.resize(levels, 8))
        for g in range(8):
            far = levels[np.abs(levels - a[p, g]) >= 10]
            a[p, g + 8] = far[np.random.randint(len(far))]
    return np.exp2(a.ravel()).repeat(32)


BF16 = ml_dtypes.bfloat16


def bf(x):
    return np.asarray(x, np.float32).astype(BF16)


def f64(x):
    return np.asarray(x).astype(np.float64)


B, S, D, H, F = 4, 1024, 1024, 16, 128
EPS = 1e-5
NTERMS = 120


def layernorm(v, gamma, beta):
    mu = v.mean(-1, keepdims=True)
    var = np.square(v - mu).mean(-1, keepdims=True)
    return (v - mu) / np.sqrt(var + EPS) * gamma + beta


def erf(z):
    z = np.clip(z, -6.0, 6.0)
    zz = 2.0 * z * z
    term = z.copy()
    tot = z.copy()
    for n in range(1, NTERMS):
        term *= zz
        term /= 2.0 * n + 1.0
        tot += term
    return 2.0 / np.sqrt(np.pi) * np.exp(-z * z) * tot


def gelu(v):
    return 0.5 * v * (1.0 + erf(v / np.sqrt(2.0)))


def setup_inputs():
    s, t = mx_kscale(D), mx_kscale(D)
    return {"attn_out": bf(0.25 * np.random.standard_normal((B, S, D)) * s),
            "x": bf(np.random.standard_normal((B, S, D)) * (0.5 + np.random.random((B, S, 1))) + 0.5 * np.random.standard_normal((B, S, 1))),
            "w_proj": bf(2.0 * np.random.standard_normal((D, D)) / np.sqrt(D) / s[:, None]),
            "b_proj": bf(0.1 * np.random.standard_normal(D)),
            "g2": bf((1.0 + 0.1 * np.random.standard_normal(D)) * t),
            "beta2": bf(0.1 * np.random.standard_normal(D) * t),
            "w_fc1": bf(np.random.standard_normal((D, F)) / np.sqrt(D) / t[:, None]),
            "b_fc1": bf(0.1 * np.random.standard_normal(F))}


def reference(attn_out, x, w_proj, b_proj, g2, beta2, w_fc1, b_fc1):
    x_mid = f64(x) + ((mxq(f64(attn_out), 2, "e4m3") @ mxq(f64(w_proj), 0, "e4m3")) + f64(b_proj))
    h = layernorm(x_mid, f64(g2), f64(beta2))
    hid = gelu((mxq(h, 2, "e4m3") @ mxq(f64(w_fc1), 0, "e4m3")) + f64(b_fc1))
    return x_mid, hid

@@ -1,0 +1,332 @@
+from contextlib import ExitStack
+
+import concourse.mybir as mybir
+from concourse.masks import make_identity
+
+F32 = mybir.dt.float32
+BF16 = mybir.dt.bfloat16
+U32 = mybir.dt.uint32
+U8 = mybir.dt.uint8
+FP8X4 = mybir.dt.float8_e4m3fn_x4
+ALU = mybir.AluOpType
+ACT = mybir.ActivationFunctionType
+
+P = 128
+PACK = 4
+K_PASS = P * PACK
+TOKENS = 4 * 1024
+D = 1024
+F = 128
+PASSES = D // K_PASS
+BANK = 512
+BANKS = 8
+HALVES = D // BANK
+BLOCKS = D // P
+TILES = TOKENS // P
+RUN = 4
+PAIR = 2
+PAIRS = TILES // PAIR
+STEPS = 9
+AHEAD = 2
+EPS = 1e-5
+
+FLOPS = 2 * TOKENS * D * D + 2 * TOKENS * D * F
+
+
+def tile_flashinferblock_pb_t_kernel(
+    tc, attn_out, x, w_proj, b_proj, g2, beta2, w_fc1, b_fc1, out_0, out_1
+):
+    nc = tc.nc
+    attn_view = attn_out.flatten_outer_dims().rearrange("(p i) d -> p i d", i=TILES)
+    x_view = x.flatten_outer_dims().rearrange("(p i) d -> p i d", i=TILES)
+    x_mid_view = out_0.flatten_outer_dims().rearrange("(p i) d -> p i d", i=TILES)
+    hid_view = out_1.flatten_outer_dims().rearrange("(p i) f -> p i f", i=TILES)
+
+    with ExitStack() as ctx:
+        const = ctx.enter_context(tc.tile_pool(name="const", bufs=1))
+        loads = ctx.enter_context(tc.tile_pool(name="loads", bufs=AHEAD + 2))
+        work = ctx.enter_context(tc.tile_pool(name="work", bufs=3))
+        stats = ctx.enter_context(tc.tile_pool(name="stats", bufs=4))
+        psum_const = ctx.enter_context(tc.psum_pool(name="psum_const", bufs=1))
+        psum = ctx.enter_context(tc.psum_pool(name="psum", bufs=BANKS - HALVES))
+        ctx.enter_context(tc.manual_schedule())
+
+        attn_sb, x_sb, a_grouped, a_codes, a_scales, x_bias, x_mid = {}, {}, {}, {}, {}, {}, {}
+        half_sums, neg_mean, inv_std, z, h_t, h_grouped, h_codes, h_scales, hid_biased = {}, {}, {}, {}, {}, {}, {}, {}, {}
+
+        def bank(shape):
+            return psum.tile(shape, F32, name="bank")
+
+        def regroup(copy, grouped, planes):
+            copy(
+                out=grouped.rearrange("p (c i) t -> p c t i", i=RUN),
+                in_=planes.rearrange("p t (c i) -> p c t i", i=RUN),
+            )
+
+        def tiles_of(pair):
+            return slice(pair * PAIR, (pair + 1) * PAIR)
+
+        def load(pair):
+            attn_sb[pair] = loads.tile([P, PAIR, D], BF16, name="attn_sb")
+            nc.sync.dma_start(out=attn_sb[pair][:], in_=attn_view[:, tiles_of(pair), :])
+            x_sb[pair] = loads.tile([P, PAIR, D], BF16, name="x_sb")
+            nc.sync.dma_start(out=x_sb[pair][:], in_=x_view[:, tiles_of(pair), :])
+
+        w_raw = const.tile([P, PASSES, PACK, D], BF16)
+        for g in range(PASSES):
+            rows = w_proj[g * K_PASS : (g + 1) * K_PASS, :]
+            nc.sync.dma_start(
+                out=w_raw[:, g, :, :],
+                in_=rows.rearrange("(p t) c -> p t c", t=PACK),
+            )
+        for pair in range(AHEAD):
+            load(pair)
+
+        gain_bf16 = const.tile([P, PASSES, PACK], BF16)
+        shift_bf16 = const.tile([P, PASSES, PACK], BF16)
+        b_proj_row = const.tile([P, D], BF16)
+        nc.vector.memset(b_proj_row[:], 0.0)
+        ones = const.tile([P, P], BF16)
+        nc.vector.memset(ones[:], 1.0)
+        nc.scalar.dma_start(out=b_proj_row[0:1, :], in_=b_proj.rearrange("(o d) -> o d", o=1))
+        nc.scalar.dma_start(out=gain_bf16[:], in_=g2.rearrange("(g p t) -> p g t", p=P, t=PACK))
+        nc.scalar.dma_start(out=shift_bf16[:], in_=beta2.rearrange("(g p t) -> p g t", p=P, t=PACK))
+        f_raw = const.tile([P, PASSES, PACK, F], BF16)
+        for g in range(PASSES):
+            rows = w_fc1[g * K_PASS : (g + 1) * K_PASS, :]
+            nc.scalar.dma_start(out=f_raw[:, g, :, :], in_=rows.rearrange("(p t) n -> p t n", t=PACK))
+        b_fc1_all = const.tile([P, F], BF16)
+        nc.scalar.dma_start(out=b_fc1_all[:], in_=b_fc1.partition_broadcast(P))
+
+        ident = const.tile([P, P], F32)
+        make_identity(nc, ident[:])
+        neg_half = const.tile([P, PAIR], F32)
+        nc.vector.memset(neg_half[:], -0.5)
+
+        w_grouped = const.tile([P, PASSES, D, PACK], BF16, align_bytes=64)
+        w_codes = const.tile([P, PASSES, D], U32, align_bytes=64)
+        w_scales = const.tile([P, PASSES, D], U8, align_bytes=64)
+
+        def regroup_w(g):
+            for half in range(HALVES):
+                cols = slice(half * BANK, (half + 1) * BANK)
+                copy = nc.vector.tensor_copy if half == 0 else nc.scalar.copy
+                regroup(copy, w_grouped[:, g, cols, :], w_raw[:, g, :, cols])
+
+        regroup_w(0)
+
+        b_proj_all = []
+        for half in range(HALVES):
+            b_proj_all.append(psum_const.tile([P, BANK], F32, name="b_proj_all%d" % half))
+            nc.tensor.matmul(
+                out=b_proj_all[half][:],
+                lhsT=ones[:],
+                rhs=b_proj_row[:, half * BANK : (half + 1) * BANK],
+                start=True,
+                stop=True,
+            )
+
+        gain = const.tile([P, BLOCKS], F32)
+        nc.vector.tensor_copy(out=gain[:], in_=gain_bf16[:].rearrange("p g t -> p (g t)"))
+        shift = const.tile([P, BLOCKS], F32)
+        nc.vector.tensor_copy(out=shift[:], in_=shift_bf16[:].rearrange("p g t -> p (g t)"))
+
+        f_grouped = const.tile([P, PASSES, F, PACK], BF16, align_bytes=64)
+        for g in range(PASSES):
+            regroup(nc.vector.tensor_copy, f_grouped[:, g, :, :], f_raw[:, g, :, :])
+        f_codes = const.tile([P, PASSES, F], U32, align_bytes=64)
+        f_scales = const.tile([P, PASSES, F], U8, align_bytes=64)
+
+        regroup_w(1)
+        nc.vector.quantize_mx(
+            out=f_codes[:].rearrange("p g n -> p (g n)").bitcast(FP8X4),
+            scales=f_scales[:].rearrange("p g n -> p (g n)"),
+            in_=f_grouped[:].rearrange("p g n t -> p (g n t)"),
+        )
+        for half in range(HALVES):
+            for g in range(PASSES):
+                cols = slice(half * BANK, (half + 1) * BANK)
+                nc.vector.quantize_mx(
+                    out=w_codes[:, g, cols].bitcast(FP8X4),
+                    scales=w_scales[:, g, cols],
+                    in_=w_grouped[:, g, cols, :].rearrange("p c t -> p (c t)"),
+                )
+
+        def transpose_attn(pair):
+            a_grouped[pair] = work.tile([P, PASSES, PAIR, P, PACK], BF16, name="a_grouped", align_bytes=64)
+            a_words = a_grouped[pair][:].bitcast(F32)
+            for j in range(PAIR):
+                attn_words = attn_sb[pair][:, j, :].bitcast(F32)
+                attn_t = bank([P, PASSES * 2, P])
+                for g in range(PASSES):
+                    for w in range(2):
+                        first, end = g * 2 * P + w, (g + 1) * 2 * P
+                        nc.tensor.transpose(attn_t[:, 2 * g + w, :], attn_words[:, first:end:2], ident[:])
+                nc.scalar.copy(out=a_words[:, :, j, :, :], in_=attn_t[:].rearrange("p (g w) r -> p g r w", w=2))
+
+        def quantise_attn(pair):
+            a_codes[pair] = work.tile([P, PASSES, PAIR, P], U32, name="a_codes", align_bytes=64)
+            a_scales[pair] = work.tile([P, PASSES, PAIR, P], U8, name="a_scales", align_bytes=64)
+            nc.vector.quantize_mx(
+                out=a_codes[pair][:].rearrange("p g j r -> p (g j r)").bitcast(FP8X4),
+                scales=a_scales[pair][:].rearrange("p g j r -> p (g j r)"),
+                in_=a_grouped[pair][:].rearrange("p g j r t -> p (g j r t)"),
+            )
+
+        def add_bias(pair):
+            x_bias[pair] = work.tile([P, PAIR, D], F32, name="x_bias", bufs=2)
+            for half in range(HALVES):
+                cols = slice(half * BANK, (half + 1) * BANK)
+                nc.vector.tensor_tensor(
+                    out=x_bias[pair][:, :, cols],
+                    in0=b_proj_all[half][:].unsqueeze(1).to_broadcast([P, PAIR, BANK]),
+                    in1=x_sb[pair][:, :, cols],
+                    op=ALU.add,
+                )
+
+        def project(pair):
+            x_mid[pair] = work.tile([P, PAIR, D], F32, name="x_mid", bufs=4)
+            half_sums[pair] = stats.tile([P, PAIR, HALVES], F32, name="half_sums")
+            for j in range(PAIR):
+                for half in range(HALVES):
+                    cols = slice(half * BANK, (half + 1) * BANK)
+                    acc = bank([P, BANK])
+                    for g in range(PASSES):
+                        nc.tensor.matmul_mx(
+                            out=acc[:],
+                            lhsT=a_codes[pair][:, g, j, :].bitcast(FP8X4),
+                            lhsT_scale=a_scales[pair][:, g, j, :],
+                            rhs=w_codes[:, g, cols].bitcast(FP8X4),
+                            rhs_scale=w_scales[:, g, cols],
+                            start=(g == 0),
+                            stop=(g == PASSES - 1),
+                        )
+                    nc.vector.scalar_tensor_tensor(
+                        out=x_mid[pair][:, j, cols],
+                        in0=acc[:],
+                        scalar=1.0,
+                        in1=x_bias[pair][:, j, cols],
+                        op0=ALU.mult,
+                        op1=ALU.add,
+                        accum_out=half_sums[pair][:, j, half : half + 1],
+                    )
+            nc.sync.dma_start(out=x_mid_view[:, tiles_of(pair), :], in_=x_mid[pair][:])
+
+        def variance(pair):
+            neg_mean[pair] = stats.tile([P, PAIR], F32, name="neg_mean")
+            sum_squares = stats.tile([P, PAIR], F32)
+            for j in range(PAIR):
+                scaled_sums = stats.tile([P, HALVES], F32)
+                nc.scalar.activation(
+                    out=scaled_sums[:],
+                    in_=half_sums[pair][:, j, :],
+                    func=ACT.Copy,
+                    scale=-1.0 / D,
+                    accum_out=neg_mean[pair][:, j : j + 1],
+                )
+                squares = work.tile([P, D], BF16, bufs=1)
+                nc.scalar.activation(
+                    out=squares[:],
+                    in_=x_mid[pair][:, j, :],
+                    func=ACT.Square,
+                    bias=neg_mean[pair][:, j : j + 1],
+                    scale=1.0,
+                    accum_out=sum_squares[:, j : j + 1],
+                )
+            var_eps = stats.tile([P, PAIR], F32)
+            nc.gpsimd.tensor_scalar(
+                out=var_eps[:], in0=sum_squares[:], scalar1=1.0 / D, scalar2=EPS, op0=ALU.mult, op1=ALU.add
+            )
+            inv_std[pair] = stats.tile([P, PAIR], F32, name="inv_std")
+            nc.gpsimd.tensor_tensor(out=inv_std[pair][:], in0=var_eps[:], in1=neg_half[:], op=ALU.pow)
+
+        def normalise(pair):
+            z[pair] = work.tile([P, PAIR, D], F32, name="z")
+            for j in range(PAIR):
+                nc.gpsimd.tensor_scalar(
+                    out=z[pair][:, j, :].rearrange("p (g t q) -> p g t q", g=PASSES, t=PACK),
+                    in0=x_mid[pair][:, j, :].rearrange("p (g q t) -> p g t q", g=PASSES, t=PACK),
+                    scalar1=neg_mean[pair][:, j : j + 1],
+                    scalar2=inv_std[pair][:, j : j + 1],
+                    op0=ALU.add,
+                    op1=ALU.mult,
+                )
+
+        def regroup_h(copy, pair, g, tokens):
+            planes = h_t[pair][:, g * PACK : (g + 1) * PACK, :, :].rearrange("p t j r -> p t (j r)")
+            regroup(copy, h_grouped[pair][:, g, tokens, :], planes[:, :, tokens])
+
+        def regroup_h_vector(pair):
+            regroup_h(nc.vector.tensor_copy, pair, 0, slice(0, PAIR * P))
+            regroup_h(nc.vector.tensor_copy, pair, 1, slice(0, P))
+
+        def transpose_norm(pair):
+            h_t[pair] = work.tile([P, BLOCKS, PAIR, P], BF16, name="h_t")
+            h_grouped[pair] = work.tile([P, PASSES, PAIR * P, PACK], BF16, name="h_grouped", align_bytes=64)
+            for first in range(0, BLOCKS, 2):
+                z_t = bank([P, 2, PAIR, P])
+                for c in range(first, first + 2):
+                    for j in range(PAIR):
+                        nc.tensor.transpose(z_t[:, c - first, j, :], z[pair][:, j, c * P : (c + 1) * P], ident[:])
+                for c in range(first, first + 2):
+                    nc.scalar.activation(
+                        out=h_t[pair][:, c, :, :],
+                        in_=z_t[:, c - first, :, :],
+                        func=ACT.Identity,
+                        scale=gain[:, c : c + 1],
+                        bias=shift[:, c : c + 1],
+                    )
+            regroup_h(nc.scalar.copy, pair, 1, slice(P, PAIR * P))
+
+        def quantise_h(pair):
+            h_codes[pair] = work.tile([P, PASSES, PAIR, P], U32, name="h_codes", align_bytes=64)
+            h_scales[pair] = work.tile([P, PASSES, PAIR, P], U8, name="h_scales", align_bytes=64)
+            nc.vector.quantize_mx(
+                out=h_codes[pair][:].rearrange("p g j r -> p (g j r)").bitcast(FP8X4),
+                scales=h_scales[pair][:].rearrange("p g j r -> p (g j r)"),
+                in_=h_grouped[pair][:].rearrange("p g r t -> p (g r t)"),
+            )
+
+        def second_product(pair):
+            hid_ps = bank([P, PAIR, F])
+            for j in range(PAIR):
+                for g in range(PASSES):
+                    nc.tensor.matmul_mx(
+                        out=hid_ps[:, j, :],
+                        lhsT=h_codes[pair][:, g, j, :].bitcast(FP8X4),
+                        lhsT_scale=h_scales[pair][:, g, j, :],
+                        rhs=f_codes[:, g, :].bitcast(FP8X4),
+                        rhs_scale=f_scales[:, g, :],
+                        start=(g == 0),
+                        stop=(g == PASSES - 1),
+                    )
+            hid_biased[pair] = work.tile([P, PAIR, F], F32, name="hid_biased")
+            nc.vector.tensor_tensor(
+                out=hid_biased[pair][:],
+                in0=hid_ps[:],
+                in1=b_fc1_all[:].unsqueeze(1).to_broadcast([P, PAIR, F]),
+                op=ALU.add,
+            )
+
+        def finish(pair):
+            hid_sb = work.tile([P, PAIR, F], F32)
+            nc.scalar.activation(out=hid_sb[:], in_=hid_biased[pair][:], func=ACT.Gelu)
+            nc.sync.dma_start(out=hid_view[:, tiles_of(pair), :], in_=hid_sb[:])
+
+        def step(function, pair):
+            if 0 <= pair < PAIRS:
+                function(pair)
+
+        for m in range(PAIRS + STEPS - 1):
+            step(load, m + AHEAD)
+            step(project, m - 2)
+            step(finish, m - 8)
+            step(variance, m - 3)
+            step(normalise, m - 3)
+            step(regroup_h_vector, m - 6)
+            step(quantise_attn, m - 1)
+            step(transpose_norm, m - 5)
+            step(quantise_h, m - 6)
+            step(add_bias, m - 1)
+            step(transpose_attn, m)
+            step(second_product, m - 7)

@@ -241,11 +241,11 @@ def tile_flashinferblock_pb_t_kernel(
             nc.gpsimd.tensor_tensor(out=inv_std[pair][:], in0=var_eps[:], in1=neg_half[:], op=ALU.pow)
 
         def normalise(pair):
-            z[pair] = work.tile([P, PAIR, D], F32, name="z")
+            z[pair] = work.tile([P, PACK, PAIR, D // PACK], F32, name="z")
             for j in range(PAIR):
                 nc.gpsimd.tensor_scalar(
-                    out=z[pair][:, j, :].rearrange("p (g t q) -> p g t q", g=PASSES, t=PACK),
-                    in0=x_mid[pair][:, j, :].rearrange("p (g q t) -> p g t q", g=PASSES, t=PACK),
+                    out=z[pair][:, :, j, :].rearrange("p t (b i) -> p b t i", i=RUN),
+                    in0=x_mid[pair][:, j, :].rearrange("p (b i t) -> p b t i", i=RUN, t=PACK),
                     scalar1=neg_mean[pair][:, j : j + 1],
                     scalar2=inv_std[pair][:, j : j + 1],
                     op0=ALU.add,
@@ -267,7 +267,9 @@ def tile_flashinferblock_pb_t_kernel(
                 z_t = bank([P, 2, PAIR, P])
                 for c in range(first, first + 2):
                     for j in range(PAIR):
-                        nc.tensor.transpose(z_t[:, c - first, j, :], z[pair][:, j, c * P : (c + 1) * P], ident[:])
+                        g, t = divmod(c, PACK)
+                        cols = slice(g * P, (g + 1) * P)
+                        nc.tensor.transpose(z_t[:, c - first, j, :], z[pair][:, t, j, cols], ident[:])
                 for c in range(first, first + 2):
                     nc.scalar.activation(
                         out=h_t[pair][:, c, :, :],

@@ -26,8 +26,8 @@ TILES = TOKENS // P
 RUN = 4
 PAIR = 2
 PAIRS = TILES // PAIR
-STEPS = 9
-AHEAD = 2
+STEPS = 5
+AHEAD = 3
 EPS = 1e-5
 
 FLOPS = 2 * TOKENS * D * D + 2 * TOKENS * D * F
@@ -44,7 +44,7 @@ def tile_flashinferblock_pb_t_kernel(
 
     with ExitStack() as ctx:
         const = ctx.enter_context(tc.tile_pool(name="const", bufs=1))
-        loads = ctx.enter_context(tc.tile_pool(name="loads", bufs=AHEAD + 2))
+        loads = ctx.enter_context(tc.tile_pool(name="loads", bufs=AHEAD + 1))
         work = ctx.enter_context(tc.tile_pool(name="work", bufs=3))
         stats = ctx.enter_context(tc.tile_pool(name="stats", bufs=4))
         psum_const = ctx.enter_context(tc.psum_pool(name="psum_const", bufs=1))
@@ -52,7 +52,8 @@ def tile_flashinferblock_pb_t_kernel(
         ctx.enter_context(tc.manual_schedule())
 
         attn_sb, x_sb, a_grouped, a_codes, a_scales, x_bias, x_mid = {}, {}, {}, {}, {}, {}, {}
-        half_sums, neg_mean, inv_std, z, h_t, h_grouped, h_codes, h_scales, hid_biased = {}, {}, {}, {}, {}, {}, {}, {}, {}
+        half_sums, neg_mean, sum_squares, var_eps, inv_std, z, h_t, h_grouped, h_codes = {}, {}, {}, {}, {}, {}, {}, {}, {}
+        h_scales, hid_biased = {}, {}
 
         def bank(shape):
             return psum.tile(shape, F32, name="bank")
@@ -67,11 +68,18 @@ def tile_flashinferblock_pb_t_kernel(
             return slice(pair * PAIR, (pair + 1) * PAIR)
 
         def load(pair):
+            load_attn(pair)
+            load_x(pair)
+
+        def load_attn(pair):
             attn_sb[pair] = loads.tile([P, PAIR, D], BF16, name="attn_sb")
             nc.sync.dma_start(out=attn_sb[pair][:], in_=attn_view[:, tiles_of(pair), :])
+
+        def load_x(pair):
             x_sb[pair] = loads.tile([P, PAIR, D], BF16, name="x_sb")
             nc.sync.dma_start(out=x_sb[pair][:], in_=x_view[:, tiles_of(pair), :])
 
+        load_attn(0)
         w_raw = const.tile([P, PASSES, PACK, D], BF16)
         for g in range(PASSES):
             rows = w_proj[g * K_PASS : (g + 1) * K_PASS, :]
@@ -79,7 +87,8 @@ def tile_flashinferblock_pb_t_kernel(
                 out=w_raw[:, g, :, :],
                 in_=rows.rearrange("(p t) c -> p t c", t=PACK),
             )
-        for pair in range(AHEAD):
+        load_x(0)
+        for pair in range(1, AHEAD):
             load(pair)
 
         gain_bf16 = const.tile([P, PASSES, PACK], BF16)
@@ -102,6 +111,40 @@ def tile_flashinferblock_pb_t_kernel(
         make_identity(nc, ident[:])
         neg_half = const.tile([P, PAIR], F32)
         nc.vector.memset(neg_half[:], -0.5)
+
+        def transpose_attn(pair):
+            a_grouped[pair] = work.tile([P, PASSES, PAIR, P, PACK], BF16, name="a_grouped", align_bytes=64)
+            a_words = a_grouped[pair][:].bitcast(F32)
+            for j in range(PAIR):
+                attn_words = attn_sb[pair][:, j, :].bitcast(F32)
+                attn_t = bank([P, PASSES * 2, P])
+                for g in range(PASSES):
+                    for w in range(2):
+                        first, end = g * 2 * P + w, (g + 1) * 2 * P
+                        nc.tensor.transpose(attn_t[:, 2 * g + w, :], attn_words[:, first:end:2], ident[:])
+                nc.scalar.copy(out=a_words[:, :, j, :, :], in_=attn_t[:].rearrange("p (g w) r -> p g r w", w=2))
+
+        def quantise_attn(pair):
+            a_codes[pair] = work.tile([P, PASSES, PAIR, P], U32, name="a_codes", align_bytes=64)
+            a_scales[pair] = work.tile([P, PASSES, PAIR, P], U8, name="a_scales", align_bytes=64)
+            nc.vector.quantize_mx(
+                out=a_codes[pair][:].rearrange("p g j r -> p (g j r)").bitcast(FP8X4),
+                scales=a_scales[pair][:].rearrange("p g j r -> p (g j r)"),
+                in_=a_grouped[pair][:].rearrange("p g j r t -> p (g j r t)"),
+            )
+
+        def add_bias(pair):
+            x_bias[pair] = work.tile([P, PAIR, D], F32, name="x_bias", bufs=2)
+            for half in range(HALVES):
+                cols = slice(half * BANK, (half + 1) * BANK)
+                nc.vector.tensor_tensor(
+                    out=x_bias[pair][:, :, cols],
+                    in0=b_proj_all[half][:].unsqueeze(1).to_broadcast([P, PAIR, BANK]),
+                    in1=x_sb[pair][:, :, cols],
+                    op=ALU.add,
+                )
+
+        transpose_attn(0)
 
         w_grouped = const.tile([P, PASSES, D, PACK], BF16, align_bytes=64)
         w_codes = const.tile([P, PASSES, D], U32, align_bytes=64)
@@ -137,6 +180,9 @@ def tile_flashinferblock_pb_t_kernel(
         f_codes = const.tile([P, PASSES, F], U32, align_bytes=64)
         f_scales = const.tile([P, PASSES, F], U8, align_bytes=64)
 
+        quantise_attn(0)
+        add_bias(0)
+
         regroup_w(1)
         nc.vector.quantize_mx(
             out=f_codes[:].rearrange("p g n -> p (g n)").bitcast(FP8X4),
@@ -150,38 +196,6 @@ def tile_flashinferblock_pb_t_kernel(
                     out=w_codes[:, g, cols].bitcast(FP8X4),
                     scales=w_scales[:, g, cols],
                     in_=w_grouped[:, g, cols, :].rearrange("p c t -> p (c t)"),
-                )
-
-        def transpose_attn(pair):
-            a_grouped[pair] = work.tile([P, PASSES, PAIR, P, PACK], BF16, name="a_grouped", align_bytes=64)
-            a_words = a_grouped[pair][:].bitcast(F32)
-            for j in range(PAIR):
-                attn_words = attn_sb[pair][:, j, :].bitcast(F32)
-                attn_t = bank([P, PASSES * 2, P])
-                for g in range(PASSES):
-                    for w in range(2):
-                        first, end = g * 2 * P + w, (g + 1) * 2 * P
-                        nc.tensor.transpose(attn_t[:, 2 * g + w, :], attn_words[:, first:end:2], ident[:])
-                nc.scalar.copy(out=a_words[:, :, j, :, :], in_=attn_t[:].rearrange("p (g w) r -> p g r w", w=2))
-
-        def quantise_attn(pair):
-            a_codes[pair] = work.tile([P, PASSES, PAIR, P], U32, name="a_codes", align_bytes=64)
-            a_scales[pair] = work.tile([P, PASSES, PAIR, P], U8, name="a_scales", align_bytes=64)
-            nc.vector.quantize_mx(
-                out=a_codes[pair][:].rearrange("p g j r -> p (g j r)").bitcast(FP8X4),
-                scales=a_scales[pair][:].rearrange("p g j r -> p (g j r)"),
-                in_=a_grouped[pair][:].rearrange("p g j r t -> p (g j r t)"),
-            )
-
-        def add_bias(pair):
-            x_bias[pair] = work.tile([P, PAIR, D], F32, name="x_bias", bufs=2)
-            for half in range(HALVES):
-                cols = slice(half * BANK, (half + 1) * BANK)
-                nc.vector.tensor_tensor(
-                    out=x_bias[pair][:, :, cols],
-                    in0=b_proj_all[half][:].unsqueeze(1).to_broadcast([P, PAIR, BANK]),
-                    in1=x_sb[pair][:, :, cols],
-                    op=ALU.add,
                 )
 
         def project(pair):
@@ -214,7 +228,7 @@ def tile_flashinferblock_pb_t_kernel(
 
         def variance(pair):
             neg_mean[pair] = stats.tile([P, PAIR], F32, name="neg_mean")
-            sum_squares = stats.tile([P, PAIR], F32)
+            sum_squares[pair] = stats.tile([P, PAIR], F32, name="sum_squares")
             for j in range(PAIR):
                 scaled_sums = stats.tile([P, HALVES], F32)
                 nc.scalar.activation(
@@ -231,16 +245,18 @@ def tile_flashinferblock_pb_t_kernel(
                     func=ACT.Square,
                     bias=neg_mean[pair][:, j : j + 1],
                     scale=1.0,
-                    accum_out=sum_squares[:, j : j + 1],
+                    accum_out=sum_squares[pair][:, j : j + 1],
                 )
-            var_eps = stats.tile([P, PAIR], F32)
-            nc.gpsimd.tensor_scalar(
-                out=var_eps[:], in0=sum_squares[:], scalar1=1.0 / D, scalar2=EPS, op0=ALU.mult, op1=ALU.add
+
+        def finish_variance(pair):
+            var_eps[pair] = stats.tile([P, PAIR], F32, name="var_eps")
+            nc.vector.tensor_scalar(
+                out=var_eps[pair][:], in0=sum_squares[pair][:], scalar1=1.0 / D, scalar2=EPS, op0=ALU.mult, op1=ALU.add
             )
-            inv_std[pair] = stats.tile([P, PAIR], F32, name="inv_std")
-            nc.gpsimd.tensor_tensor(out=inv_std[pair][:], in0=var_eps[:], in1=neg_half[:], op=ALU.pow)
 
         def normalise(pair):
+            inv_std[pair] = stats.tile([P, PAIR], F32, name="inv_std")
+            nc.gpsimd.tensor_tensor(out=inv_std[pair][:], in0=var_eps[pair][:], in1=neg_half[:], op=ALU.pow)
             z[pair] = work.tile([P, PACK, PAIR, D // PACK], F32, name="z")
             for j in range(PAIR):
                 nc.gpsimd.tensor_scalar(
@@ -252,13 +268,23 @@ def tile_flashinferblock_pb_t_kernel(
                     op1=ALU.mult,
                 )
 
-        def regroup_h(copy, pair, g, tokens):
-            planes = h_t[pair][:, g * PACK : (g + 1) * PACK, :, :].rearrange("p t j r -> p t (j r)")
-            regroup(copy, h_grouped[pair][:, g, tokens, :], planes[:, :, tokens])
+        def planes_of_h(pair, g, tokens):
+            return h_t[pair][:, g * PACK : (g + 1) * PACK, :, :].rearrange("p t j r -> p t (j r)")[:, :, tokens]
+
+        def regroup_h_gpsimd(pair):
+            for g, tokens in ((0, slice(0, PAIR * P)), (1, slice(0, P))):
+                nc.gpsimd.tensor_scalar(
+                    out=h_grouped[pair][:, g, tokens, :],
+                    in0=planes_of_h(pair, g, tokens).rearrange("p t r -> p r t"),
+                    scalar1=1.0,
+                    scalar2=0.0,
+                    op0=ALU.mult,
+                    op1=ALU.add,
+                )
 
         def regroup_h_vector(pair):
-            regroup_h(nc.vector.tensor_copy, pair, 0, slice(0, PAIR * P))
-            regroup_h(nc.vector.tensor_copy, pair, 1, slice(0, P))
+            tokens = slice(P, PAIR * P)
+            regroup(nc.vector.tensor_copy, h_grouped[pair][:, 1, tokens, :], planes_of_h(pair, 1, tokens))
 
         def transpose_norm(pair):
             h_t[pair] = work.tile([P, BLOCKS, PAIR, P], BF16, name="h_t")
@@ -278,7 +304,6 @@ def tile_flashinferblock_pb_t_kernel(
                         scale=gain[:, c : c + 1],
                         bias=shift[:, c : c + 1],
                     )
-            regroup_h(nc.scalar.copy, pair, 1, slice(P, PAIR * P))
 
         def quantise_h(pair):
             h_codes[pair] = work.tile([P, PASSES, PAIR, P], U32, name="h_codes", align_bytes=64)
@@ -321,14 +346,16 @@ def tile_flashinferblock_pb_t_kernel(
 
         for m in range(PAIRS + STEPS - 1):
             step(load, m + AHEAD)
-            step(project, m - 2)
-            step(finish, m - 8)
-            step(variance, m - 3)
-            step(normalise, m - 3)
-            step(regroup_h_vector, m - 6)
-            step(quantise_attn, m - 1)
-            step(transpose_norm, m - 5)
-            step(quantise_h, m - 6)
-            step(add_bias, m - 1)
-            step(transpose_attn, m)
-            step(second_product, m - 7)
+            step(transpose_norm, m - 2)
+            step(project, m)
+            step(transpose_attn, m + 1)
+            step(finish, m - 4)
+            step(variance, m)
+            step(normalise, m - 1)
+            step(regroup_h_gpsimd, m - 2)
+            step(add_bias, m + 1)
+            step(quantise_attn, m + 1)
+            step(regroup_h_vector, m - 2)
+            step(second_product, m - 3)
+            step(quantise_h, m - 2)
+            step(finish_variance, m)

@@ -26,8 +26,9 @@ TILES = TOKENS // P
 RUN = 4
 PAIR = 2
 PAIRS = TILES // PAIR
-STEPS = 5
+STEPS = 4
 AHEAD = 3
+GROUP = 4
 EPS = 1e-5
 
 FLOPS = 2 * TOKENS * D * D + 2 * TOKENS * D * F
@@ -44,7 +45,7 @@ def tile_flashinferblock_pb_t_kernel(
 
     with ExitStack() as ctx:
         const = ctx.enter_context(tc.tile_pool(name="const", bufs=1))
-        loads = ctx.enter_context(tc.tile_pool(name="loads", bufs=AHEAD + 1))
+        loads = ctx.enter_context(tc.tile_pool(name="loads", bufs=AHEAD))
         work = ctx.enter_context(tc.tile_pool(name="work", bufs=3))
         stats = ctx.enter_context(tc.tile_pool(name="stats", bufs=4))
         psum_const = ctx.enter_context(tc.psum_pool(name="psum_const", bufs=1))
@@ -52,8 +53,8 @@ def tile_flashinferblock_pb_t_kernel(
         ctx.enter_context(tc.manual_schedule())
 
         attn_sb, x_sb, a_grouped, a_codes, a_scales, x_bias, x_mid = {}, {}, {}, {}, {}, {}, {}
-        half_sums, neg_mean, sum_squares, var_eps, inv_std, z, h_t, h_grouped, h_codes = {}, {}, {}, {}, {}, {}, {}, {}, {}
-        h_scales, hid_biased = {}, {}
+        half_sums, neg_mean, std, inv_std, z, h_t, h_grouped, h_codes, h_scales = {}, {}, {}, {}, {}, {}, {}, {}, {}
+        hid = {}
 
         def bank(shape):
             return psum.tile(shape, F32, name="bank")
@@ -79,7 +80,11 @@ def tile_flashinferblock_pb_t_kernel(
             x_sb[pair] = loads.tile([P, PAIR, D], BF16, name="x_sb")
             nc.sync.dma_start(out=x_sb[pair][:], in_=x_view[:, tiles_of(pair), :])
 
+        b_proj_row = const.tile([P, D], BF16)
+        nc.vector.memset(b_proj_row[:], 0.0)
         load_attn(0)
+        nc.sync.dma_start(out=b_proj_row[0:1, :], in_=b_proj.rearrange("(o d) -> o d", o=1))
+        load_x(0)
         w_raw = const.tile([P, PASSES, PACK, D], BF16)
         for g in range(PASSES):
             rows = w_proj[g * K_PASS : (g + 1) * K_PASS, :]
@@ -87,17 +92,13 @@ def tile_flashinferblock_pb_t_kernel(
                 out=w_raw[:, g, :, :],
                 in_=rows.rearrange("(p t) c -> p t c", t=PACK),
             )
-        load_x(0)
         for pair in range(1, AHEAD):
             load(pair)
 
         gain_bf16 = const.tile([P, PASSES, PACK], BF16)
         shift_bf16 = const.tile([P, PASSES, PACK], BF16)
-        b_proj_row = const.tile([P, D], BF16)
-        nc.vector.memset(b_proj_row[:], 0.0)
         ones = const.tile([P, P], BF16)
         nc.vector.memset(ones[:], 1.0)
-        nc.scalar.dma_start(out=b_proj_row[0:1, :], in_=b_proj.rearrange("(o d) -> o d", o=1))
         nc.scalar.dma_start(out=gain_bf16[:], in_=g2.rearrange("(g p t) -> p g t", p=P, t=PACK))
         nc.scalar.dma_start(out=shift_bf16[:], in_=beta2.rearrange("(g p t) -> p g t", p=P, t=PACK))
         f_raw = const.tile([P, PASSES, PACK, F], BF16)
@@ -107,10 +108,13 @@ def tile_flashinferblock_pb_t_kernel(
         b_fc1_all = const.tile([P, F], BF16)
         nc.scalar.dma_start(out=b_fc1_all[:], in_=b_fc1.partition_broadcast(P))
 
+        eps = const.tile([P, 1], F32)
+        nc.vector.memset(eps[:], EPS)
+        eps_root = const.tile([P, 1], F32)
+        nc.scalar.activation(out=eps_root[:], in_=eps[:], func=ACT.Sqrt)
+
         ident = const.tile([P, P], F32)
         make_identity(nc, ident[:])
-        neg_half = const.tile([P, PAIR], F32)
-        nc.vector.memset(neg_half[:], -0.5)
 
         def transpose_attn(pair):
             a_grouped[pair] = work.tile([P, PASSES, PAIR, P, PACK], BF16, name="a_grouped", align_bytes=64)
@@ -146,18 +150,6 @@ def tile_flashinferblock_pb_t_kernel(
 
         transpose_attn(0)
 
-        w_grouped = const.tile([P, PASSES, D, PACK], BF16, align_bytes=64)
-        w_codes = const.tile([P, PASSES, D], U32, align_bytes=64)
-        w_scales = const.tile([P, PASSES, D], U8, align_bytes=64)
-
-        def regroup_w(g):
-            for half in range(HALVES):
-                cols = slice(half * BANK, (half + 1) * BANK)
-                copy = nc.vector.tensor_copy if half == 0 else nc.scalar.copy
-                regroup(copy, w_grouped[:, g, cols, :], w_raw[:, g, :, cols])
-
-        regroup_w(0)
-
         b_proj_all = []
         for half in range(HALVES):
             b_proj_all.append(psum_const.tile([P, BANK], F32, name="b_proj_all%d" % half))
@@ -168,6 +160,9 @@ def tile_flashinferblock_pb_t_kernel(
                 start=True,
                 stop=True,
             )
+
+        quantise_attn(0)
+        add_bias(0)
 
         gain = const.tile([P, BLOCKS], F32)
         nc.vector.tensor_copy(out=gain[:], in_=gain_bf16[:].rearrange("p g t -> p (g t)"))
@@ -180,10 +175,18 @@ def tile_flashinferblock_pb_t_kernel(
         f_codes = const.tile([P, PASSES, F], U32, align_bytes=64)
         f_scales = const.tile([P, PASSES, F], U8, align_bytes=64)
 
-        quantise_attn(0)
-        add_bias(0)
+        w_grouped = const.tile([P, PASSES, D, PACK], BF16, align_bytes=64)
+        w_codes = const.tile([P, PASSES, D], U32, align_bytes=64)
+        w_scales = const.tile([P, PASSES, D], U8, align_bytes=64)
 
-        regroup_w(1)
+        def regroup_w(g):
+            for half in range(HALVES):
+                cols = slice(half * BANK, (half + 1) * BANK)
+                copy = nc.vector.tensor_copy if half == 0 else nc.scalar.copy
+                regroup(copy, w_grouped[:, g, cols, :], w_raw[:, g, :, cols])
+
+        for g in range(PASSES):
+            regroup_w(g)
         nc.vector.quantize_mx(
             out=f_codes[:].rearrange("p g n -> p (g n)").bitcast(FP8X4),
             scales=f_scales[:].rearrange("p g n -> p (g n)"),
@@ -228,7 +231,7 @@ def tile_flashinferblock_pb_t_kernel(
 
         def variance(pair):
             neg_mean[pair] = stats.tile([P, PAIR], F32, name="neg_mean")
-            sum_squares[pair] = stats.tile([P, PAIR], F32, name="sum_squares")
+            sum_squares = stats.tile([P, PAIR], F32)
             for j in range(PAIR):
                 scaled_sums = stats.tile([P, HALVES], F32)
                 nc.scalar.activation(
@@ -245,21 +248,20 @@ def tile_flashinferblock_pb_t_kernel(
                     func=ACT.Square,
                     bias=neg_mean[pair][:, j : j + 1],
                     scale=1.0,
-                    accum_out=sum_squares[pair][:, j : j + 1],
+                    accum_out=sum_squares[:, j : j + 1],
                 )
+            std[pair] = stats.tile([P, PAIR], F32, name="std")
+            nc.scalar.activation(out=std[pair][:], in_=sum_squares[:], func=ACT.Sqrt, scale=1.0 / D, bias=eps[:])
 
-        def finish_variance(pair):
-            var_eps[pair] = stats.tile([P, PAIR], F32, name="var_eps")
-            nc.vector.tensor_scalar(
-                out=var_eps[pair][:], in0=sum_squares[pair][:], scalar1=1.0 / D, scalar2=EPS, op0=ALU.mult, op1=ALU.add
-            )
+        def invert_std(pair):
+            inv_std[pair] = stats.tile([P, PAIR], F32, name="inv_std")
+            nc.vector.reciprocal(out=inv_std[pair][:], in_=std[pair][:])
 
         def normalise(pair):
-            inv_std[pair] = stats.tile([P, PAIR], F32, name="inv_std")
-            nc.gpsimd.tensor_tensor(out=inv_std[pair][:], in0=var_eps[pair][:], in1=neg_half[:], op=ALU.pow)
+            engine = nc.vector if pair == PAIRS - 1 else nc.gpsimd
             z[pair] = work.tile([P, PACK, PAIR, D // PACK], F32, name="z")
             for j in range(PAIR):
-                nc.gpsimd.tensor_scalar(
+                engine.tensor_scalar(
                     out=z[pair][:, :, j, :].rearrange("p t (b i) -> p b t i", i=RUN),
                     in0=x_mid[pair][:, j, :].rearrange("p (b i t) -> p b t i", i=RUN, t=PACK),
                     scalar1=neg_mean[pair][:, j : j + 1],
@@ -268,23 +270,21 @@ def tile_flashinferblock_pb_t_kernel(
                     op1=ALU.mult,
                 )
 
-        def planes_of_h(pair, g, tokens):
-            return h_t[pair][:, g * PACK : (g + 1) * PACK, :, :].rearrange("p t j r -> p t (j r)")[:, :, tokens]
+        def planes_of_h(pair, g):
+            return h_t[pair][:, g * PACK : (g + 1) * PACK, :, :].rearrange("p t j r -> p t (j r)")
 
         def regroup_h_gpsimd(pair):
-            for g, tokens in ((0, slice(0, PAIR * P)), (1, slice(0, P))):
-                nc.gpsimd.tensor_scalar(
-                    out=h_grouped[pair][:, g, tokens, :],
-                    in0=planes_of_h(pair, g, tokens).rearrange("p t r -> p r t"),
-                    scalar1=1.0,
-                    scalar2=0.0,
-                    op0=ALU.mult,
-                    op1=ALU.add,
-                )
+            nc.gpsimd.tensor_scalar(
+                out=h_grouped[pair][:, 0, :, :],
+                in0=planes_of_h(pair, 0).rearrange("p t r -> p r t"),
+                scalar1=1.0,
+                scalar2=0.0,
+                op0=ALU.mult,
+                op1=ALU.add,
+            )
 
-        def regroup_h_vector(pair):
-            tokens = slice(P, PAIR * P)
-            regroup(nc.vector.tensor_copy, h_grouped[pair][:, 1, tokens, :], planes_of_h(pair, 1, tokens))
+        def regroup_h_vector(pair, g):
+            regroup(nc.vector.tensor_copy, h_grouped[pair][:, g, :, :], planes_of_h(pair, g))
 
         def transpose_norm(pair):
             h_t[pair] = work.tile([P, BLOCKS, PAIR, P], BF16, name="h_t")
@@ -327,35 +327,43 @@ def tile_flashinferblock_pb_t_kernel(
                         start=(g == 0),
                         stop=(g == PASSES - 1),
                     )
-            hid_biased[pair] = work.tile([P, PAIR, F], F32, name="hid_biased")
+            group, first = divmod(pair * PAIR, GROUP * PAIR)
+            if first == 0:
+                hid[group] = const.tile([P, GROUP * PAIR, F], F32, name="hid%d" % group)
             nc.vector.tensor_tensor(
-                out=hid_biased[pair][:],
+                out=hid[group][:, first : first + PAIR, :],
                 in0=hid_ps[:],
                 in1=b_fc1_all[:].unsqueeze(1).to_broadcast([P, PAIR, F]),
                 op=ALU.add,
             )
 
-        def finish(pair):
-            hid_sb = work.tile([P, PAIR, F], F32)
-            nc.scalar.activation(out=hid_sb[:], in_=hid_biased[pair][:], func=ACT.Gelu)
-            nc.sync.dma_start(out=hid_view[:, tiles_of(pair), :], in_=hid_sb[:])
+        def finish(group):
+            tiles = slice(group * GROUP * PAIR, (group + 1) * GROUP * PAIR)
+            nc.scalar.activation(out=hid[group][:], in_=hid[group][:], func=ACT.Gelu)
+            nc.sync.dma_start(out=hid_view[:, tiles, :], in_=hid[group][:])
 
-        def step(function, pair):
+        def step(function, pair, *args):
             if 0 <= pair < PAIRS:
-                function(pair)
+                function(pair, *args)
 
         for m in range(PAIRS + STEPS - 1):
             step(load, m + AHEAD)
             step(transpose_norm, m - 2)
+            step(invert_std, m - 1)
+            step(quantise_h, m - 3)
             step(project, m)
-            step(transpose_attn, m + 1)
-            step(finish, m - 4)
-            step(variance, m)
-            step(normalise, m - 1)
-            step(regroup_h_gpsimd, m - 2)
             step(add_bias, m + 1)
-            step(quantise_attn, m + 1)
-            step(regroup_h_vector, m - 2)
+            step(normalise, m - 1)
+            if m - 2 >= PAIRS - 2:
+                step(regroup_h_vector, m - 2, 0)
+            else:
+                step(regroup_h_gpsimd, m - 2)
+            for pair in range(1 if m == 0 else m + 2, m + 3):
+                step(transpose_attn, pair)
+            step(variance, m)
             step(second_product, m - 3)
-            step(quantise_h, m - 2)
-            step(finish_variance, m)
+            step(regroup_h_vector, m - 2, 1)
+            for pair in range(1 if m == 0 else m + 2, m + 3):
+                step(quantise_attn, pair)
+        for group in range(PAIRS // GROUP):
+            finish(group)

@@ -26,7 +26,6 @@ TILES = TOKENS // P
 RUN = 4
 PAIR = 2
 PAIRS = TILES // PAIR
-STEPS = 4
 AHEAD = 3
 GROUP = 4
 EPS = 1e-5
@@ -53,8 +52,8 @@ def tile_flashinferblock_pb_t_kernel(
         ctx.enter_context(tc.manual_schedule())
 
         attn_sb, x_sb, a_grouped, a_codes, a_scales, x_bias, x_mid = {}, {}, {}, {}, {}, {}, {}
-        half_sums, neg_mean, std, inv_std, z, h_t, h_grouped, h_codes, h_scales = {}, {}, {}, {}, {}, {}, {}, {}, {}
-        hid = {}
+        half_sums, neg_mean, std, inv_std, z, z_t, h_t, h_grouped, h_codes = {}, {}, {}, {}, {}, {}, {}, {}, {}
+        sum_squares, h_scales, hid = {}, {}, {}
 
         def bank(shape):
             return psum.tile(shape, F32, name="bank")
@@ -229,29 +228,35 @@ def tile_flashinferblock_pb_t_kernel(
                     )
             nc.sync.dma_start(out=x_mid_view[:, tiles_of(pair), :], in_=x_mid[pair][:])
 
-        def variance(pair):
-            neg_mean[pair] = stats.tile([P, PAIR], F32, name="neg_mean")
-            sum_squares = stats.tile([P, PAIR], F32)
-            for j in range(PAIR):
-                scaled_sums = stats.tile([P, HALVES], F32)
-                nc.scalar.activation(
-                    out=scaled_sums[:],
-                    in_=half_sums[pair][:, j, :],
-                    func=ACT.Copy,
-                    scale=-1.0 / D,
-                    accum_out=neg_mean[pair][:, j : j + 1],
-                )
-                squares = work.tile([P, D], BF16, bufs=1)
-                nc.scalar.activation(
-                    out=squares[:],
-                    in_=x_mid[pair][:, j, :],
-                    func=ACT.Square,
-                    bias=neg_mean[pair][:, j : j + 1],
-                    scale=1.0,
-                    accum_out=sum_squares[:, j : j + 1],
-                )
+        def mean(pair, j):
+            if j == 0:
+                neg_mean[pair] = stats.tile([P, PAIR], F32, name="neg_mean")
+                sum_squares[pair] = stats.tile([P, PAIR], F32, name="sum_squares")
+            scaled_sums = stats.tile([P, HALVES], F32)
+            nc.scalar.activation(
+                out=scaled_sums[:],
+                in_=half_sums[pair][:, j, :],
+                func=ACT.Copy,
+                scale=-1.0 / D,
+                accum_out=neg_mean[pair][:, j : j + 1],
+            )
+
+        def square(pair, j):
+            squares = work.tile([P, D], BF16, bufs=1)
+            nc.scalar.activation(
+                out=squares[:],
+                in_=x_mid[pair][:, j, :],
+                func=ACT.Square,
+                bias=neg_mean[pair][:, j : j + 1],
+                scale=1.0,
+                accum_out=sum_squares[pair][:, j : j + 1],
+            )
+
+        def root(pair):
             std[pair] = stats.tile([P, PAIR], F32, name="std")
-            nc.scalar.activation(out=std[pair][:], in_=sum_squares[:], func=ACT.Sqrt, scale=1.0 / D, bias=eps[:])
+            nc.scalar.activation(
+                out=std[pair][:], in_=sum_squares[pair][:], func=ACT.Sqrt, scale=1.0 / D, bias=eps[:]
+            )
 
         def invert_std(pair):
             inv_std[pair] = stats.tile([P, PAIR], F32, name="inv_std")
@@ -270,40 +275,44 @@ def tile_flashinferblock_pb_t_kernel(
                     op1=ALU.mult,
                 )
 
-        def planes_of_h(pair, g):
-            return h_t[pair][:, g * PACK : (g + 1) * PACK, :, :].rearrange("p t j r -> p t (j r)")
+        def planes_of_h(pair, g, tokens):
+            return h_t[pair][:, g * PACK : (g + 1) * PACK, :, :].rearrange("p t j r -> p t (j r)")[:, :, tokens]
 
-        def regroup_h_gpsimd(pair):
+        def regroup_h_gpsimd(pair, g, tokens):
             nc.gpsimd.tensor_scalar(
-                out=h_grouped[pair][:, 0, :, :],
-                in0=planes_of_h(pair, 0).rearrange("p t r -> p r t"),
+                out=h_grouped[pair][:, g, tokens, :],
+                in0=planes_of_h(pair, g, tokens).rearrange("p t r -> p r t"),
                 scalar1=1.0,
                 scalar2=0.0,
                 op0=ALU.mult,
                 op1=ALU.add,
             )
 
-        def regroup_h_vector(pair, g):
-            regroup(nc.vector.tensor_copy, h_grouped[pair][:, g, :, :], planes_of_h(pair, g))
+        def regroup_h_vector(pair, g, tokens):
+            regroup(nc.vector.tensor_copy, h_grouped[pair][:, g, tokens, :], planes_of_h(pair, g, tokens))
 
         def transpose_norm(pair):
-            h_t[pair] = work.tile([P, BLOCKS, PAIR, P], BF16, name="h_t")
-            h_grouped[pair] = work.tile([P, PASSES, PAIR * P, PACK], BF16, name="h_grouped", align_bytes=64)
+            z_t[pair] = []
             for first in range(0, BLOCKS, 2):
-                z_t = bank([P, 2, PAIR, P])
+                z_t[pair].append(bank([P, 2, PAIR, P]))
                 for c in range(first, first + 2):
                     for j in range(PAIR):
                         g, t = divmod(c, PACK)
                         cols = slice(g * P, (g + 1) * P)
-                        nc.tensor.transpose(z_t[:, c - first, j, :], z[pair][:, t, j, cols], ident[:])
-                for c in range(first, first + 2):
-                    nc.scalar.activation(
-                        out=h_t[pair][:, c, :, :],
-                        in_=z_t[:, c - first, :, :],
-                        func=ACT.Identity,
-                        scale=gain[:, c : c + 1],
-                        bias=shift[:, c : c + 1],
+                        nc.tensor.transpose(z_t[pair][-1][:, c - first, j, :], z[pair][:, t, j, cols], ident[:])
+            h_t[pair] = work.tile([P, BLOCKS, PAIR, P], BF16, name="h_t")
+            h_grouped[pair] = work.tile([P, PASSES, PAIR * P, PACK], BF16, name="h_grouped", align_bytes=64)
+
+        def shift_norm(pair, blocks, on_vector=False):
+            for c in blocks:
+                out, in_ = h_t[pair][:, c, :, :], z_t[pair][c // 2][:, c % 2, :, :]
+                scale, bias = gain[:, c : c + 1], shift[:, c : c + 1]
+                if on_vector:
+                    nc.vector.tensor_scalar(
+                        out=out, in0=in_, scalar1=scale, scalar2=bias, op0=ALU.mult, op1=ALU.add
                     )
+                else:
+                    nc.scalar.activation(out=out, in_=in_, func=ACT.Identity, scale=scale, bias=bias)
 
         def quantise_h(pair):
             h_codes[pair] = work.tile([P, PASSES, PAIR, P], U32, name="h_codes", align_bytes=64)
@@ -337,33 +346,62 @@ def tile_flashinferblock_pb_t_kernel(
                 op=ALU.add,
             )
 
-        def finish(group):
-            tiles = slice(group * GROUP * PAIR, (group + 1) * GROUP * PAIR)
-            nc.scalar.activation(out=hid[group][:], in_=hid[group][:], func=ACT.Gelu)
-            nc.sync.dma_start(out=hid_view[:, tiles, :], in_=hid[group][:])
+        def finish(pairs):
+            group, first = divmod(pairs.start, GROUP)
+            part = hid[group][:, first * PAIR : (first + len(pairs)) * PAIR, :]
+            nc.scalar.activation(out=part, in_=part, func=ACT.Gelu)
+            nc.sync.dma_start(out=hid_view[:, pairs.start * PAIR : pairs.stop * PAIR, :], in_=part)
 
         def step(function, pair, *args):
             if 0 <= pair < PAIRS:
                 function(pair, *args)
 
-        for m in range(PAIRS + STEPS - 1):
+        all_tokens, first_tile, second_tile = slice(0, PAIR * P), slice(0, P), slice(P, PAIR * P)
+        all_blocks, first_blocks, last_blocks = range(BLOCKS), range(BLOCKS // 2), range(BLOCKS // 2, BLOCKS)
+        last = PAIRS - 1
+        for m in range(PAIRS):
             step(load, m + AHEAD)
             step(transpose_norm, m - 2)
-            step(invert_std, m - 1)
+            step(shift_norm, m - 2, all_blocks)
             step(quantise_h, m - 3)
-            step(project, m)
-            step(add_bias, m + 1)
+            if m > 0:
+                step(quantise_attn, m + 1)
+            step(invert_std, m - 1)
+            project(m)
             step(normalise, m - 1)
-            if m - 2 >= PAIRS - 2:
-                step(regroup_h_vector, m - 2, 0)
-            else:
-                step(regroup_h_gpsimd, m - 2)
+            step(regroup_h_gpsimd, m - 2, 0, all_tokens)
+            if m < last:
+                step(regroup_h_gpsimd, m - 2, 1, first_tile)
+            mean(m, 0)
+            square(m, 0)
+            mean(m, 1)
             for pair in range(1 if m == 0 else m + 2, m + 3):
                 step(transpose_attn, pair)
-            step(variance, m)
+            square(m, 1)
+            root(m)
+            step(add_bias, m + 1)
+            if m == 0:
+                quantise_attn(1)
             step(second_product, m - 3)
-            step(regroup_h_vector, m - 2, 1)
-            for pair in range(1 if m == 0 else m + 2, m + 3):
-                step(quantise_attn, pair)
-        for group in range(PAIRS // GROUP):
-            finish(group)
+            step(regroup_h_vector, m - 2, 1, second_tile if m < last else all_tokens)
+
+        transpose_norm(last - 1)
+        shift_norm(last - 1, all_blocks)
+        invert_std(last)
+        normalise(last)
+        quantise_h(last - 2)
+        transpose_norm(last)
+        for g in range(PASSES):
+            regroup_h_vector(last - 1, g, all_tokens)
+        shift_norm(last, last_blocks, on_vector=True)
+        shift_norm(last, first_blocks)
+        quantise_h(last - 1)
+        for g in reversed(range(PASSES)):
+            regroup_h_vector(last, g, all_tokens)
+        second_product(last - 2)
+        second_product(last - 1)
+        for first in range(0, last, GROUP):
+            finish(range(first, min(first + GROUP, last)))
+        quantise_h(last)
+        second_product(last)
+        finish(range(last, PAIRS))

@@ -48,7 +48,7 @@ def tile_flashinferblock_pb_t_kernel(
         work = ctx.enter_context(tc.tile_pool(name="work", bufs=3))
         stats = ctx.enter_context(tc.tile_pool(name="stats", bufs=4))
         psum_const = ctx.enter_context(tc.psum_pool(name="psum_const", bufs=1))
-        psum = ctx.enter_context(tc.psum_pool(name="psum", bufs=BANKS - HALVES))
+        psum = ctx.enter_context(tc.psum_pool(name="psum", bufs=BANKS - 1))
         ctx.enter_context(tc.manual_schedule())
 
         attn_sb, x_sb, a_grouped, a_codes, a_scales, x_bias, x_mid = {}, {}, {}, {}, {}, {}, {}
@@ -138,26 +138,20 @@ def tile_flashinferblock_pb_t_kernel(
 
         def add_bias(pair):
             x_bias[pair] = work.tile([P, PAIR, D], F32, name="x_bias", bufs=2)
-            for half in range(HALVES):
-                cols = slice(half * BANK, (half + 1) * BANK)
-                nc.vector.tensor_tensor(
-                    out=x_bias[pair][:, :, cols],
-                    in0=b_proj_all[half][:].unsqueeze(1).to_broadcast([P, PAIR, BANK]),
-                    in1=x_sb[pair][:, :, cols],
-                    op=ALU.add,
-                )
+            nc.vector.tensor_tensor(
+                out=x_bias[pair][:],
+                in0=b_proj_all[:].unsqueeze(1).to_broadcast([P, PAIR, D]),
+                in1=x_sb[pair][:],
+                op=ALU.add,
+            )
 
         transpose_attn(0)
 
-        b_proj_all = []
+        b_proj_all = psum_const.tile([P, D], BF16)
         for half in range(HALVES):
-            b_proj_all.append(psum_const.tile([P, BANK], F32, name="b_proj_all%d" % half))
+            cols = slice(half * BANK, (half + 1) * BANK)
             nc.tensor.matmul(
-                out=b_proj_all[half][:],
-                lhsT=ones[:],
-                rhs=b_proj_row[:, half * BANK : (half + 1) * BANK],
-                start=True,
-                stop=True,
+                out=b_proj_all[:, cols], lhsT=ones[:], rhs=b_proj_row[:, cols], start=True, stop=True
             )
 
         quantise_attn(0)
@@ -200,33 +194,34 @@ def tile_flashinferblock_pb_t_kernel(
                     in_=w_grouped[:, g, cols, :].rearrange("p c t -> p (c t)"),
                 )
 
-        def project(pair):
-            x_mid[pair] = work.tile([P, PAIR, D], F32, name="x_mid", bufs=4)
-            half_sums[pair] = stats.tile([P, PAIR, HALVES], F32, name="half_sums")
-            for j in range(PAIR):
-                for half in range(HALVES):
-                    cols = slice(half * BANK, (half + 1) * BANK)
-                    acc = bank([P, BANK])
-                    for g in range(PASSES):
-                        nc.tensor.matmul_mx(
-                            out=acc[:],
-                            lhsT=a_codes[pair][:, g, j, :].bitcast(FP8X4),
-                            lhsT_scale=a_scales[pair][:, g, j, :],
-                            rhs=w_codes[:, g, cols].bitcast(FP8X4),
-                            rhs_scale=w_scales[:, g, cols],
-                            start=(g == 0),
-                            stop=(g == PASSES - 1),
-                        )
-                    nc.vector.scalar_tensor_tensor(
-                        out=x_mid[pair][:, j, cols],
-                        in0=acc[:],
-                        scalar=1.0,
-                        in1=x_bias[pair][:, j, cols],
-                        op0=ALU.mult,
-                        op1=ALU.add,
-                        accum_out=half_sums[pair][:, j, half : half + 1],
+        def project(pair, j):
+            if j == 0:
+                x_mid[pair] = work.tile([P, PAIR, D], F32, name="x_mid")
+                half_sums[pair] = stats.tile([P, PAIR, HALVES], F32, name="half_sums")
+            for half in range(HALVES):
+                cols = slice(half * BANK, (half + 1) * BANK)
+                acc = bank([P, BANK])
+                for g in range(PASSES):
+                    nc.tensor.matmul_mx(
+                        out=acc[:],
+                        lhsT=a_codes[pair][:, g, j, :].bitcast(FP8X4),
+                        lhsT_scale=a_scales[pair][:, g, j, :],
+                        rhs=w_codes[:, g, cols].bitcast(FP8X4),
+                        rhs_scale=w_scales[:, g, cols],
+                        start=(g == 0),
+                        stop=(g == PASSES - 1),
                     )
-            nc.sync.dma_start(out=x_mid_view[:, tiles_of(pair), :], in_=x_mid[pair][:])
+                nc.vector.scalar_tensor_tensor(
+                    out=x_mid[pair][:, j, cols],
+                    in0=acc[:],
+                    scalar=1.0,
+                    in1=x_bias[pair][:, j, cols],
+                    op0=ALU.mult,
+                    op1=ALU.add,
+                    accum_out=half_sums[pair][:, j, half : half + 1],
+                )
+            if j == PAIR - 1:
+                nc.sync.dma_start(out=x_mid_view[:, tiles_of(pair), :], in_=x_mid[pair][:])
 
         def mean(pair, j):
             if j == 0:
@@ -242,7 +237,7 @@ def tile_flashinferblock_pb_t_kernel(
             )
 
         def square(pair, j):
-            squares = work.tile([P, D], BF16, bufs=1)
+            squares = work.tile([P, D], BF16)
             nc.scalar.activation(
                 out=squares[:],
                 in_=x_mid[pair][:, j, :],
@@ -263,7 +258,7 @@ def tile_flashinferblock_pb_t_kernel(
             nc.vector.reciprocal(out=inv_std[pair][:], in_=std[pair][:])
 
         def normalise(pair):
-            engine = nc.vector if pair == PAIRS - 1 else nc.gpsimd
+            engine = nc.vector if pair >= PAIRS - 2 else nc.gpsimd
             z[pair] = work.tile([P, PACK, PAIR, D // PACK], F32, name="z")
             for j in range(PAIR):
                 engine.tensor_scalar(
@@ -275,21 +270,20 @@ def tile_flashinferblock_pb_t_kernel(
                     op1=ALU.mult,
                 )
 
-        def planes_of_h(pair, g, tokens):
-            return h_t[pair][:, g * PACK : (g + 1) * PACK, :, :].rearrange("p t j r -> p t (j r)")[:, :, tokens]
+        def regroup_h(copy, pair, g, tokens):
+            planes = h_t[pair][:, g * PACK : (g + 1) * PACK, :, :].rearrange("p t j r -> p t (j r)")
+            regroup(copy, h_grouped[pair][:, g, tokens, :], planes[:, :, tokens])
 
-        def regroup_h_gpsimd(pair, g, tokens):
-            nc.gpsimd.tensor_scalar(
-                out=h_grouped[pair][:, g, tokens, :],
-                in0=planes_of_h(pair, g, tokens).rearrange("p t r -> p r t"),
-                scalar1=1.0,
-                scalar2=0.0,
-                op0=ALU.mult,
-                op1=ALU.add,
-            )
+        def regroup_h_vector(pair):
+            regroup_h(nc.vector.tensor_copy, pair, 0, slice(0, PAIR * P))
+            regroup_h(nc.vector.tensor_copy, pair, 1, slice(0, P))
 
-        def regroup_h_vector(pair, g, tokens):
-            regroup(nc.vector.tensor_copy, h_grouped[pair][:, g, tokens, :], planes_of_h(pair, g, tokens))
+        def regroup_h_scalar(pair):
+            regroup_h(nc.scalar.copy, pair, 1, slice(P, PAIR * P))
+
+        def regroup_h_whole(pair):
+            for g in range(PASSES):
+                regroup_h(nc.vector.tensor_copy, pair, g, slice(0, PAIR * P))
 
         def transpose_norm(pair):
             z_t[pair] = []
@@ -356,52 +350,60 @@ def tile_flashinferblock_pb_t_kernel(
             if 0 <= pair < PAIRS:
                 function(pair, *args)
 
-        all_tokens, first_tile, second_tile = slice(0, PAIR * P), slice(0, P), slice(P, PAIR * P)
         all_blocks, first_blocks, last_blocks = range(BLOCKS), range(BLOCKS // 2), range(BLOCKS // 2, BLOCKS)
-        last = PAIRS - 1
         for m in range(PAIRS):
             step(load, m + AHEAD)
-            step(transpose_norm, m - 2)
-            step(shift_norm, m - 2, all_blocks)
-            step(quantise_h, m - 3)
-            if m > 0:
-                step(quantise_attn, m + 1)
-            step(invert_std, m - 1)
-            project(m)
-            step(normalise, m - 1)
-            step(regroup_h_gpsimd, m - 2, 0, all_tokens)
-            if m < last:
-                step(regroup_h_gpsimd, m - 2, 1, first_tile)
-            mean(m, 0)
-            square(m, 0)
-            mean(m, 1)
+            step(invert_std, m - 2)
+            step(normalise, m - 2)
+            step(transpose_norm, m - 3)
+            for function in (mean, square):
+                for j in range(PAIR):
+                    step(function, m - 1, j)
+            step(add_bias, m + 1)
+            project(m, 0)
+            step(shift_norm, m - 3, first_blocks)
+            step(root, m - 1)
+            step(shift_norm, m - 3, last_blocks)
+            step(quantise_h, m - 5)
+            step(regroup_h_vector, m - 4)
+            step(regroup_h_scalar, m - 4)
+            project(m, 1)
+            step(second_product, m - 5)
             for pair in range(1 if m == 0 else m + 2, m + 3):
                 step(transpose_attn, pair)
-            square(m, 1)
-            root(m)
-            step(add_bias, m + 1)
-            if m == 0:
-                quantise_attn(1)
-            step(second_product, m - 3)
-            step(regroup_h_vector, m - 2, 1, second_tile if m < last else all_tokens)
+            step(quantise_attn, m + 1)
 
-        transpose_norm(last - 1)
-        shift_norm(last - 1, all_blocks)
+        last = PAIRS - 1
+        for function in (mean, square):
+            for j in range(PAIR):
+                function(last, j)
+        root(last)
+        invert_std(last - 1)
+        normalise(last - 1)
+        transpose_norm(last - 2)
+        shift_norm(last - 2, all_blocks)
+        quantise_h(last - 4)
+        regroup_h_whole(last - 3)
         invert_std(last)
         normalise(last)
-        quantise_h(last - 2)
+        transpose_norm(last - 1)
+        shift_norm(last - 1, all_blocks)
+        second_product(last - 4)
+        quantise_h(last - 3)
         transpose_norm(last)
-        for g in range(PASSES):
-            regroup_h_vector(last - 1, g, all_tokens)
-        shift_norm(last, last_blocks, on_vector=True)
-        shift_norm(last, first_blocks)
+        regroup_h_whole(last - 2)
+        shift_norm(last, range(2, BLOCKS), on_vector=True)
+        shift_norm(last, range(2))
+        second_product(last - 3)
+        quantise_h(last - 2)
+        regroup_h_whole(last - 1)
+        regroup_h_whole(last)
+        for first in range(0, PAIRS - GROUP, GROUP):
+            finish(range(first, first + GROUP))
         quantise_h(last - 1)
-        for g in reversed(range(PASSES)):
-            regroup_h_vector(last, g, all_tokens)
         second_product(last - 2)
-        second_product(last - 1)
-        for first in range(0, last, GROUP):
-            finish(range(first, min(first + GROUP, last)))
         quantise_h(last)
+        second_product(last - 1)
+        finish(range(PAIRS - GROUP, last))
         second_product(last)
         finish(range(last, PAIRS))

@@ -80,10 +80,10 @@ def tile_flashinferblock_pb_t_kernel(
             nc.sync.dma_start(out=x_sb[pair][:], in_=x_view[:, tiles_of(pair), :])
 
         b_proj_row = const.tile([P, D], BF16)
-        nc.vector.memset(b_proj_row[:], 0.0)
-        load_attn(0)
-        nc.sync.dma_start(out=b_proj_row[0:1, :], in_=b_proj.rearrange("(o d) -> o d", o=1))
+        nc.vector.memset(b_proj_row[:].bitcast(F32), 0.0)
         load_x(0)
+        nc.sync.dma_start(out=b_proj_row[0:1, :], in_=b_proj.rearrange("(o d) -> o d", o=1))
+        load_attn(0)
         w_raw = const.tile([P, PASSES, PACK, D], BF16)
         for g in range(PASSES):
             rows = w_proj[g * K_PASS : (g + 1) * K_PASS, :]
@@ -145,8 +145,6 @@ def tile_flashinferblock_pb_t_kernel(
                 op=ALU.add,
             )
 
-        transpose_attn(0)
-
         b_proj_all = psum_const.tile([P, D], BF16)
         for half in range(HALVES):
             cols = slice(half * BANK, (half + 1) * BANK)
@@ -154,45 +152,56 @@ def tile_flashinferblock_pb_t_kernel(
                 out=b_proj_all[:, cols], lhsT=ones[:], rhs=b_proj_row[:, cols], start=True, stop=True
             )
 
-        quantise_attn(0)
         add_bias(0)
+        transpose_attn(0)
 
         gain = const.tile([P, BLOCKS], F32)
-        nc.vector.tensor_copy(out=gain[:], in_=gain_bf16[:].rearrange("p g t -> p (g t)"))
+        nc.gpsimd.tensor_copy(out=gain[:], in_=gain_bf16[:].rearrange("p g t -> p (g t)"))
         shift = const.tile([P, BLOCKS], F32)
-        nc.vector.tensor_copy(out=shift[:], in_=shift_bf16[:].rearrange("p g t -> p (g t)"))
-
+        nc.gpsimd.tensor_copy(out=shift[:], in_=shift_bf16[:].rearrange("p g t -> p (g t)"))
         f_grouped = const.tile([P, PASSES, F, PACK], BF16, align_bytes=64)
         for g in range(PASSES):
-            regroup(nc.vector.tensor_copy, f_grouped[:, g, :, :], f_raw[:, g, :, :])
+            nc.gpsimd.tensor_scalar(
+                out=f_grouped[:, g, :, :],
+                in0=f_raw[:, g, :, :].rearrange("p t n -> p n t"),
+                scalar1=1.0,
+                scalar2=0.0,
+                op0=ALU.mult,
+                op1=ALU.add,
+            )
         f_codes = const.tile([P, PASSES, F], U32, align_bytes=64)
         f_scales = const.tile([P, PASSES, F], U8, align_bytes=64)
+
+        def quantise_f():
+            nc.vector.quantize_mx(
+                out=f_codes[:].rearrange("p g n -> p (g n)").bitcast(FP8X4),
+                scales=f_scales[:].rearrange("p g n -> p (g n)"),
+                in_=f_grouped[:].rearrange("p g n t -> p (g n t)"),
+            )
 
         w_grouped = const.tile([P, PASSES, D, PACK], BF16, align_bytes=64)
         w_codes = const.tile([P, PASSES, D], U32, align_bytes=64)
         w_scales = const.tile([P, PASSES, D], U8, align_bytes=64)
+        halves = [slice(half * BANK, (half + 1) * BANK) for half in range(HALVES)]
 
         def regroup_w(g):
-            for half in range(HALVES):
-                cols = slice(half * BANK, (half + 1) * BANK)
-                copy = nc.vector.tensor_copy if half == 0 else nc.scalar.copy
+            for copy, cols in zip((nc.vector.tensor_copy, nc.scalar.copy), halves):
                 regroup(copy, w_grouped[:, g, cols, :], w_raw[:, g, :, cols])
 
-        for g in range(PASSES):
-            regroup_w(g)
-        nc.vector.quantize_mx(
-            out=f_codes[:].rearrange("p g n -> p (g n)").bitcast(FP8X4),
-            scales=f_scales[:].rearrange("p g n -> p (g n)"),
-            in_=f_grouped[:].rearrange("p g n t -> p (g n t)"),
-        )
-        for half in range(HALVES):
-            for g in range(PASSES):
-                cols = slice(half * BANK, (half + 1) * BANK)
-                nc.vector.quantize_mx(
-                    out=w_codes[:, g, cols].bitcast(FP8X4),
-                    scales=w_scales[:, g, cols],
-                    in_=w_grouped[:, g, cols, :].rearrange("p c t -> p (c t)"),
-                )
+        def quantise_w(g, cols):
+            nc.vector.quantize_mx(
+                out=w_codes[:, g, cols].bitcast(FP8X4),
+                scales=w_scales[:, g, cols],
+                in_=w_grouped[:, g, cols, :].rearrange("p c t -> p (c t)"),
+            )
+
+        regroup_w(0)
+        quantise_attn(0)
+        quantise_w(0, halves[0])
+        regroup_w(1)
+        quantise_w(0, halves[1])
+        for cols in halves:
+            quantise_w(1, cols)
 
         def project(pair, j):
             if j == 0:
@@ -368,6 +377,8 @@ def tile_flashinferblock_pb_t_kernel(
             step(regroup_h_vector, m - 4)
             step(regroup_h_scalar, m - 4)
             project(m, 1)
+            if m == 0:
+                quantise_f()
             step(second_product, m - 5)
             for pair in range(1 if m == 0 else m + 2, m + 3):
                 step(transpose_attn, pair)

@@ -53,10 +53,10 @@ def tile_flashinferblock_pb_t_kernel(
 
         attn_sb, x_sb, a_grouped, a_codes, a_scales, x_bias, x_mid = {}, {}, {}, {}, {}, {}, {}
         half_sums, neg_mean, std, inv_std, z, z_t, h_t, h_grouped, h_codes = {}, {}, {}, {}, {}, {}, {}, {}, {}
-        sum_squares, h_scales, hid = {}, {}, {}
+        sum_squares, words, h_scales, hid = {}, {}, {}, {}
 
-        def bank(shape):
-            return psum.tile(shape, F32, name="bank")
+        def bank(shape, dtype=F32):
+            return psum.tile(shape, dtype, name="bank")
 
         def regroup(copy, grouped, planes):
             copy(
@@ -114,6 +114,8 @@ def tile_flashinferblock_pb_t_kernel(
 
         ident = const.tile([P, P], F32)
         make_identity(nc, ident[:])
+        ident_bf16 = const.tile([P, P], BF16)
+        make_identity(nc, ident_bf16[:])
 
         def transpose_attn(pair):
             a_grouped[pair] = work.tile([P, PASSES, PAIR, P, PACK], BF16, name="a_grouped", align_bytes=64)
@@ -285,10 +287,22 @@ def tile_flashinferblock_pb_t_kernel(
 
         def regroup_h_vector(pair):
             regroup_h(nc.vector.tensor_copy, pair, 0, slice(0, PAIR * P))
-            regroup_h(nc.vector.tensor_copy, pair, 1, slice(0, P))
+
+        def regroup_h_tensor(pair):
+            words[pair] = bank([P, PAIR, P, PACK], BF16)
+            for j in range(PAIR):
+                nc.tensor.matmul(
+                    out=words[pair][:, j, :, :],
+                    lhsT=ident_bf16[:],
+                    rhs=h_t[pair][:, PACK : 2 * PACK, j, :].rearrange("p t r -> p r t"),
+                    start=True,
+                    stop=True,
+                )
 
         def regroup_h_scalar(pair):
-            regroup_h(nc.scalar.copy, pair, 1, slice(P, PAIR * P))
+            nc.scalar.copy(
+                out=h_grouped[pair][:, 1, :, :].rearrange("p (j r) t -> p j r t", j=PAIR), in_=words[pair][:]
+            )
 
         def regroup_h_whole(pair):
             for g in range(PASSES):
@@ -362,29 +376,35 @@ def tile_flashinferblock_pb_t_kernel(
         all_blocks, first_blocks, last_blocks = range(BLOCKS), range(BLOCKS // 2), range(BLOCKS // 2, BLOCKS)
         for m in range(PAIRS):
             step(load, m + AHEAD)
-            step(invert_std, m - 2)
-            step(normalise, m - 2)
+            if m > 0:
+                step(quantise_attn, m + 1)
             step(transpose_norm, m - 3)
-            for function in (mean, square):
-                for j in range(PAIR):
-                    step(function, m - 1, j)
-            step(add_bias, m + 1)
-            project(m, 0)
+            step(mean, m - 1, 0)
             step(shift_norm, m - 3, first_blocks)
-            step(root, m - 1)
+            step(mean, m - 1, 1)
             step(shift_norm, m - 3, last_blocks)
             step(quantise_h, m - 5)
             step(regroup_h_vector, m - 4)
-            step(regroup_h_scalar, m - 4)
+            step(invert_std, m - 2)
+            step(normalise, m - 2)
+            step(add_bias, m + 1)
+            project(m, 0)
+            for j in range(PAIR):
+                step(square, m - 1, j)
             project(m, 1)
-            if m == 0:
-                quantise_f()
             step(second_product, m - 5)
             for pair in range(1 if m == 0 else m + 2, m + 3):
                 step(transpose_attn, pair)
-            step(quantise_attn, m + 1)
+            step(regroup_h_tensor, m - 4)
+            step(regroup_h_scalar, m - 4)
+            step(root, m - 1)
+            if m == 0:
+                quantise_attn(1)
+                quantise_f()
 
         last = PAIRS - 1
+        regroup_h_whole(last - 3)
+        quantise_h(last - 4)
         for function in (mean, square):
             for j in range(PAIR):
                 function(last, j)
@@ -393,14 +413,12 @@ def tile_flashinferblock_pb_t_kernel(
         normalise(last - 1)
         transpose_norm(last - 2)
         shift_norm(last - 2, all_blocks)
-        quantise_h(last - 4)
-        regroup_h_whole(last - 3)
+        second_product(last - 4)
+        quantise_h(last - 3)
         invert_std(last)
         normalise(last)
         transpose_norm(last - 1)
         shift_norm(last - 1, all_blocks)
-        second_product(last - 4)
-        quantise_h(last - 3)
         transpose_norm(last)
         regroup_h_whole(last - 2)
         shift_norm(last, range(2, BLOCKS), on_vector=True)

from contextlib import ExitStack

import concourse.mybir as mybir
from concourse.masks import make_identity

F32 = mybir.dt.float32
BF16 = mybir.dt.bfloat16
U32 = mybir.dt.uint32
U8 = mybir.dt.uint8
FP8X4 = mybir.dt.float8_e4m3fn_x4
ALU = mybir.AluOpType
ACT = mybir.ActivationFunctionType

P = 128
PACK = 4
K_PASS = P * PACK
TOKENS = 4 * 1024
D = 1024
F = 128
PASSES = D // K_PASS
BANK = 512
BANKS = 8
HALVES = D // BANK
BLOCKS = D // P
TILES = TOKENS // P
RUN = 4
PAIR = 2
PAIRS = TILES // PAIR
AHEAD = 3
GROUP = 4
EPS = 1e-5

FLOPS = 2 * TOKENS * D * D + 2 * TOKENS * D * F


def tile_flashinferblock_pb_t_kernel(
    tc, attn_out, x, w_proj, b_proj, g2, beta2, w_fc1, b_fc1, out_0, out_1
):
    nc = tc.nc
    attn_view = attn_out.flatten_outer_dims().rearrange("(p i) d -> p i d", i=TILES)
    x_view = x.flatten_outer_dims().rearrange("(p i) d -> p i d", i=TILES)
    x_mid_view = out_0.flatten_outer_dims().rearrange("(p i) d -> p i d", i=TILES)
    hid_view = out_1.flatten_outer_dims().rearrange("(p i) f -> p i f", i=TILES)

    with ExitStack() as ctx:
        const = ctx.enter_context(tc.tile_pool(name="const", bufs=1))
        loads = ctx.enter_context(tc.tile_pool(name="loads", bufs=AHEAD))
        work = ctx.enter_context(tc.tile_pool(name="work", bufs=3))
        stats = ctx.enter_context(tc.tile_pool(name="stats", bufs=4))
        psum_const = ctx.enter_context(tc.psum_pool(name="psum_const", bufs=1))
        psum = ctx.enter_context(tc.psum_pool(name="psum", bufs=BANKS - 1))
        ctx.enter_context(tc.manual_schedule())

        attn_sb, x_sb, a_grouped, a_codes, a_scales, x_bias, x_mid = {}, {}, {}, {}, {}, {}, {}
        half_sums, neg_mean, std, inv_std, z, z_t, h_t, h_grouped, h_codes = {}, {}, {}, {}, {}, {}, {}, {}, {}
        sum_squares, words, h_scales, hid = {}, {}, {}, {}

        def bank(shape, dtype=F32):
            return psum.tile(shape, dtype, name="bank")

        def regroup(copy, grouped, planes):
            copy(
                out=grouped.rearrange("p (c i) t -> p c t i", i=RUN),
                in_=planes.rearrange("p t (c i) -> p c t i", i=RUN),
            )

        def tiles_of(pair):
            return slice(pair * PAIR, (pair + 1) * PAIR)

        def load(pair):
            load_attn(pair)
            load_x(pair)

        def load_attn(pair):
            attn_sb[pair] = loads.tile([P, PAIR, D], BF16, name="attn_sb")
            nc.sync.dma_start(out=attn_sb[pair][:], in_=attn_view[:, tiles_of(pair), :])

        def load_x(pair):
            x_sb[pair] = loads.tile([P, PAIR, D], BF16, name="x_sb")
            nc.sync.dma_start(out=x_sb[pair][:], in_=x_view[:, tiles_of(pair), :])

        b_proj_row = const.tile([P, D], BF16)
        nc.vector.memset(b_proj_row[:].bitcast(F32), 0.0)
        load_x(0)
        nc.sync.dma_start(out=b_proj_row[0:1, :], in_=b_proj.rearrange("(o d) -> o d", o=1))
        load_attn(0)
        w_raw = const.tile([P, PASSES, PACK, D], BF16)
        for g in range(PASSES):
            rows = w_proj[g * K_PASS : (g + 1) * K_PASS, :]
            nc.sync.dma_start(
                out=w_raw[:, g, :, :],
                in_=rows.rearrange("(p t) c -> p t c", t=PACK),
            )
        for pair in range(1, AHEAD):
            load(pair)

        gain_bf16 = const.tile([P, PASSES, PACK], BF16)
        shift_bf16 = const.tile([P, PASSES, PACK], BF16)
        ones = const.tile([P, P], BF16)
        nc.vector.memset(ones[:], 1.0)
        nc.scalar.dma_start(out=gain_bf16[:], in_=g2.rearrange("(g p t) -> p g t", p=P, t=PACK))
        nc.scalar.dma_start(out=shift_bf16[:], in_=beta2.rearrange("(g p t) -> p g t", p=P, t=PACK))
        f_raw = const.tile([P, PASSES, PACK, F], BF16)
        for g in range(PASSES):
            rows = w_fc1[g * K_PASS : (g + 1) * K_PASS, :]
            nc.scalar.dma_start(out=f_raw[:, g, :, :], in_=rows.rearrange("(p t) n -> p t n", t=PACK))
        b_fc1_all = const.tile([P, F], BF16)
        nc.scalar.dma_start(out=b_fc1_all[:], in_=b_fc1.partition_broadcast(P))

        eps = const.tile([P, 1], F32)
        nc.vector.memset(eps[:], EPS)
        eps_root = const.tile([P, 1], F32)
        nc.scalar.activation(out=eps_root[:], in_=eps[:], func=ACT.Sqrt)

        ident = const.tile([P, P], F32)
        make_identity(nc, ident[:])
        ident_bf16 = const.tile([P, P], BF16)
        make_identity(nc, ident_bf16[:])

        def transpose_attn(pair):
            a_grouped[pair] = work.tile([P, PASSES, PAIR, P, PACK], BF16, name="a_grouped", align_bytes=64)
            a_words = a_grouped[pair][:].bitcast(F32)
            for j in range(PAIR):
                attn_words = attn_sb[pair][:, j, :].bitcast(F32)
                attn_t = bank([P, PASSES * 2, P])
                for g in range(PASSES):
                    for w in range(2):
                        first, end = g * 2 * P + w, (g + 1) * 2 * P
                        nc.tensor.transpose(attn_t[:, 2 * g + w, :], attn_words[:, first:end:2], ident[:])
                nc.scalar.copy(out=a_words[:, :, j, :, :], in_=attn_t[:].rearrange("p (g w) r -> p g r w", w=2))

        def quantise_attn(pair):
            a_codes[pair] = work.tile([P, PASSES, PAIR, P], U32, name="a_codes", align_bytes=64)
            a_scales[pair] = work.tile([P, PASSES, PAIR, P], U8, name="a_scales", align_bytes=64)
            nc.vector.quantize_mx(
                out=a_codes[pair][:].rearrange("p g j r -> p (g j r)").bitcast(FP8X4),
                scales=a_scales[pair][:].rearrange("p g j r -> p (g j r)"),
                in_=a_grouped[pair][:].rearrange("p g j r t -> p (g j r t)"),
            )

        def add_bias(pair):
            x_bias[pair] = work.tile([P, PAIR, D], F32, name="x_bias", bufs=2)
            nc.vector.tensor_tensor(
                out=x_bias[pair][:],
                in0=b_proj_all[:].unsqueeze(1).to_broadcast([P, PAIR, D]),
                in1=x_sb[pair][:],
                op=ALU.add,
            )

        b_proj_all = psum_const.tile([P, D], BF16)
        for half in range(HALVES):
            cols = slice(half * BANK, (half + 1) * BANK)
            nc.tensor.matmul(
                out=b_proj_all[:, cols], lhsT=ones[:], rhs=b_proj_row[:, cols], start=True, stop=True
            )

        add_bias(0)
        transpose_attn(0)

        gain = const.tile([P, BLOCKS], F32)
        nc.gpsimd.tensor_copy(out=gain[:], in_=gain_bf16[:].rearrange("p g t -> p (g t)"))
        shift = const.tile([P, BLOCKS], F32)
        nc.gpsimd.tensor_copy(out=shift[:], in_=shift_bf16[:].rearrange("p g t -> p (g t)"))
        f_grouped = const.tile([P, PASSES, F, PACK], BF16, align_bytes=64)
        for g in range(PASSES):
            nc.gpsimd.tensor_scalar(
                out=f_grouped[:, g, :, :],
                in0=f_raw[:, g, :, :].rearrange("p t n -> p n t"),
                scalar1=1.0,
                scalar2=0.0,
                op0=ALU.mult,
                op1=ALU.add,
            )
        f_codes = const.tile([P, PASSES, F], U32, align_bytes=64)
        f_scales = const.tile([P, PASSES, F], U8, align_bytes=64)

        def quantise_f():
            nc.vector.quantize_mx(
                out=f_codes[:].rearrange("p g n -> p (g n)").bitcast(FP8X4),
                scales=f_scales[:].rearrange("p g n -> p (g n)"),
                in_=f_grouped[:].rearrange("p g n t -> p (g n t)"),
            )

        w_grouped = const.tile([P, PASSES, D, PACK], BF16, align_bytes=64)
        w_codes = const.tile([P, PASSES, D], U32, align_bytes=64)
        w_scales = const.tile([P, PASSES, D], U8, align_bytes=64)
        halves = [slice(half * BANK, (half + 1) * BANK) for half in range(HALVES)]

        def regroup_w(g):
            for copy, cols in zip((nc.vector.tensor_copy, nc.scalar.copy), halves):
                regroup(copy, w_grouped[:, g, cols, :], w_raw[:, g, :, cols])

        def quantise_w(g, cols):
            nc.vector.quantize_mx(
                out=w_codes[:, g, cols].bitcast(FP8X4),
                scales=w_scales[:, g, cols],
                in_=w_grouped[:, g, cols, :].rearrange("p c t -> p (c t)"),
            )

        regroup_w(0)
        quantise_attn(0)
        quantise_w(0, halves[0])
        regroup_w(1)
        quantise_w(0, halves[1])
        for cols in halves:
            quantise_w(1, cols)

        def project(pair, j):
            if j == 0:
                x_mid[pair] = work.tile([P, PAIR, D], F32, name="x_mid")
                half_sums[pair] = stats.tile([P, PAIR, HALVES], F32, name="half_sums")
            for half in range(HALVES):
                cols = slice(half * BANK, (half + 1) * BANK)
                acc = bank([P, BANK])
                for g in range(PASSES):
                    nc.tensor.matmul_mx(
                        out=acc[:],
                        lhsT=a_codes[pair][:, g, j, :].bitcast(FP8X4),
                        lhsT_scale=a_scales[pair][:, g, j, :],
                        rhs=w_codes[:, g, cols].bitcast(FP8X4),
                        rhs_scale=w_scales[:, g, cols],
                        start=(g == 0),
                        stop=(g == PASSES - 1),
                    )
                nc.vector.scalar_tensor_tensor(
                    out=x_mid[pair][:, j, cols],
                    in0=acc[:],
                    scalar=1.0,
                    in1=x_bias[pair][:, j, cols],
                    op0=ALU.mult,
                    op1=ALU.add,
                    accum_out=half_sums[pair][:, j, half : half + 1],
                )
            if j == PAIR - 1:
                nc.sync.dma_start(out=x_mid_view[:, tiles_of(pair), :], in_=x_mid[pair][:])

        def mean(pair, j):
            if j == 0:
                neg_mean[pair] = stats.tile([P, PAIR], F32, name="neg_mean")
                sum_squares[pair] = stats.tile([P, PAIR], F32, name="sum_squares")
            scaled_sums = stats.tile([P, HALVES], F32)
            nc.scalar.activation(
                out=scaled_sums[:],
                in_=half_sums[pair][:, j, :],
                func=ACT.Copy,
                scale=-1.0 / D,
                accum_out=neg_mean[pair][:, j : j + 1],
            )

        def square(pair, j):
            squares = work.tile([P, D], BF16)
            nc.scalar.activation(
                out=squares[:],
                in_=x_mid[pair][:, j, :],
                func=ACT.Square,
                bias=neg_mean[pair][:, j : j + 1],
                scale=1.0,
                accum_out=sum_squares[pair][:, j : j + 1],
            )

        def root(pair):
            std[pair] = stats.tile([P, PAIR], F32, name="std")
            nc.scalar.activation(
                out=std[pair][:], in_=sum_squares[pair][:], func=ACT.Sqrt, scale=1.0 / D, bias=eps[:]
            )

        def invert_std(pair):
            inv_std[pair] = stats.tile([P, PAIR], F32, name="inv_std")
            nc.vector.reciprocal(out=inv_std[pair][:], in_=std[pair][:])

        def normalise(pair):
            engine = nc.vector if pair >= PAIRS - 2 else nc.gpsimd
            z[pair] = work.tile([P, PACK, PAIR, D // PACK], F32, name="z")
            for j in range(PAIR):
                engine.tensor_scalar(
                    out=z[pair][:, :, j, :].rearrange("p t (b i) -> p b t i", i=RUN),
                    in0=x_mid[pair][:, j, :].rearrange("p (b i t) -> p b t i", i=RUN, t=PACK),
                    scalar1=neg_mean[pair][:, j : j + 1],
                    scalar2=inv_std[pair][:, j : j + 1],
                    op0=ALU.add,
                    op1=ALU.mult,
                )

        def regroup_h(copy, pair, g, tokens):
            planes = h_t[pair][:, g * PACK : (g + 1) * PACK, :, :].rearrange("p t j r -> p t (j r)")
            regroup(copy, h_grouped[pair][:, g, tokens, :], planes[:, :, tokens])

        def regroup_h_vector(pair):
            regroup_h(nc.vector.tensor_copy, pair, 0, slice(0, PAIR * P))

        def regroup_h_tensor(pair):
            words[pair] = bank([P, PAIR, P, PACK], BF16)
            for j in range(PAIR):
                nc.tensor.matmul(
                    out=words[pair][:, j, :, :],
                    lhsT=ident_bf16[:],
                    rhs=h_t[pair][:, PACK : 2 * PACK, j, :].rearrange("p t r -> p r t"),
                    start=True,
                    stop=True,
                )

        def regroup_h_scalar(pair):
            nc.scalar.copy(
                out=h_grouped[pair][:, 1, :, :].rearrange("p (j r) t -> p j r t", j=PAIR), in_=words[pair][:]
            )

        def regroup_h_whole(pair):
            for g in range(PASSES):
                regroup_h(nc.vector.tensor_copy, pair, g, slice(0, PAIR * P))

        def transpose_norm(pair):
            z_t[pair] = []
            for first in range(0, BLOCKS, 2):
                z_t[pair].append(bank([P, 2, PAIR, P]))
                for c in range(first, first + 2):
                    for j in range(PAIR):
                        g, t = divmod(c, PACK)
                        cols = slice(g * P, (g + 1) * P)
                        nc.tensor.transpose(z_t[pair][-1][:, c - first, j, :], z[pair][:, t, j, cols], ident[:])
            h_t[pair] = work.tile([P, BLOCKS, PAIR, P], BF16, name="h_t")
            h_grouped[pair] = work.tile([P, PASSES, PAIR * P, PACK], BF16, name="h_grouped", align_bytes=64)

        def shift_norm(pair, blocks, on_vector=False):
            for c in blocks:
                out, in_ = h_t[pair][:, c, :, :], z_t[pair][c // 2][:, c % 2, :, :]
                scale, bias = gain[:, c : c + 1], shift[:, c : c + 1]
                if on_vector:
                    nc.vector.tensor_scalar(
                        out=out, in0=in_, scalar1=scale, scalar2=bias, op0=ALU.mult, op1=ALU.add
                    )
                else:
                    nc.scalar.activation(out=out, in_=in_, func=ACT.Identity, scale=scale, bias=bias)

        def quantise_h(pair):
            h_codes[pair] = work.tile([P, PASSES, PAIR, P], U32, name="h_codes", align_bytes=64)
            h_scales[pair] = work.tile([P, PASSES, PAIR, P], U8, name="h_scales", align_bytes=64)
            nc.vector.quantize_mx(
                out=h_codes[pair][:].rearrange("p g j r -> p (g j r)").bitcast(FP8X4),
                scales=h_scales[pair][:].rearrange("p g j r -> p (g j r)"),
                in_=h_grouped[pair][:].rearrange("p g r t -> p (g r t)"),
            )

        def second_product(pair):
            hid_ps = bank([P, PAIR, F])
            for j in range(PAIR):
                for g in range(PASSES):
                    nc.tensor.matmul_mx(
                        out=hid_ps[:, j, :],
                        lhsT=h_codes[pair][:, g, j, :].bitcast(FP8X4),
                        lhsT_scale=h_scales[pair][:, g, j, :],
                        rhs=f_codes[:, g, :].bitcast(FP8X4),
                        rhs_scale=f_scales[:, g, :],
                        start=(g == 0),
                        stop=(g == PASSES - 1),
                    )
            group, first = divmod(pair * PAIR, GROUP * PAIR)
            if first == 0:
                hid[group] = const.tile([P, GROUP * PAIR, F], F32, name="hid%d" % group)
            nc.vector.tensor_tensor(
                out=hid[group][:, first : first + PAIR, :],
                in0=hid_ps[:],
                in1=b_fc1_all[:].unsqueeze(1).to_broadcast([P, PAIR, F]),
                op=ALU.add,
            )

        def finish(pairs):
            group, first = divmod(pairs.start, GROUP)
            part = hid[group][:, first * PAIR : (first + len(pairs)) * PAIR, :]
            nc.scalar.activation(out=part, in_=part, func=ACT.Gelu)
            nc.sync.dma_start(out=hid_view[:, pairs.start * PAIR : pairs.stop * PAIR, :], in_=part)

        def step(function, pair, *args):
            if 0 <= pair < PAIRS:
                function(pair, *args)

        all_blocks, first_blocks, last_blocks = range(BLOCKS), range(BLOCKS // 2), range(BLOCKS // 2, BLOCKS)
        for m in range(PAIRS):
            step(load, m + AHEAD)
            if m > 0:
                step(quantise_attn, m + 1)
            step(transpose_norm, m - 3)
            step(mean, m - 1, 0)
            step(shift_norm, m - 3, first_blocks)
            step(mean, m - 1, 1)
            step(shift_norm, m - 3, last_blocks)
            step(quantise_h, m - 5)
            step(regroup_h_vector, m - 4)
            step(invert_std, m - 2)
            step(normalise, m - 2)
            step(add_bias, m + 1)
            project(m, 0)
            for j in range(PAIR):
                step(square, m - 1, j)
            project(m, 1)
            step(second_product, m - 5)
            for pair in range(1 if m == 0 else m + 2, m + 3):
                step(transpose_attn, pair)
            step(regroup_h_tensor, m - 4)
            step(regroup_h_scalar, m - 4)
            step(root, m - 1)
            if m == 0:
                quantise_attn(1)
                quantise_f()

        last = PAIRS - 1
        regroup_h_whole(last - 3)
        quantise_h(last - 4)
        for function in (mean, square):
            for j in range(PAIR):
                function(last, j)
        root(last)
        invert_std(last - 1)
        normalise(last - 1)
        transpose_norm(last - 2)
        shift_norm(last - 2, all_blocks)
        second_product(last - 4)
        quantise_h(last - 3)
        invert_std(last)
        normalise(last)
        transpose_norm(last - 1)
        shift_norm(last - 1, all_blocks)
        transpose_norm(last)
        regroup_h_whole(last - 2)
        shift_norm(last, range(2, BLOCKS), on_vector=True)
        shift_norm(last, range(2))
        second_product(last - 3)
        quantise_h(last - 2)
        regroup_h_whole(last - 1)
        regroup_h_whole(last)
        for first in range(0, PAIRS - GROUP, GROUP):
            finish(range(first, first + GROUP))
        quantise_h(last - 1)
        second_product(last - 2)
        quantise_h(last)
        second_product(last - 1)
        finish(range(PAIRS - GROUP, last))
        second_product(last)
        finish(range(last, PAIRS))
